import numpy as np
import ml_dtypes


def mxq(x, axis, fmt="e4m3"):
    dtype, down = {"e4m3": (ml_dtypes.float8_e4m3fn, 7), "e5m2": (ml_dtypes.float8_e5m2, 14)}[fmt]
    v = np.moveaxis(np.asarray(x, np.float32).astype(ml_dtypes.bfloat16).astype(np.float64), axis, -1)
    blocks = v.reshape(v.shape[:-1] + (-1, 32))
    amax = np.abs(blocks).max(-1, keepdims=True)
    byte = np.maximum(np.where(amax > 0, np.frexp(amax)[1] - 1 + 127, 0) - down, 1)
    scale = np.exp2(byte - 127.0)
    codes = (blocks / scale).astype(np.float32).astype(dtype).astype(np.float64)
    return np.moveaxis((codes * scale).reshape(v.shape), -1, axis)


WIDE = False


def mx_kscale(k):
    if not WIDE:
        return np.ones(k)
    levels = np.array([10, -10, 5, -5, 0])
    a = np.random.permutation(np.resize(levels, k // 512 * 4)).reshape(k // 512, 4)
    idx = np.arange(k)
    return np.exp2(a[idx // 512, idx % 128 // 32])


BF16 = ml_dtypes.bfloat16


def bf(x):
    return np.asarray(x, np.float32).astype(BF16)


def f64(x):
    return np.asarray(x).astype(np.float64)


N, X_DIM, Y_DIM, HID = 4096, 512, 128, 1024


def setup_inputs():
    s = mx_kscale(X_DIM)
    t, u = mx_kscale(HID), mx_kscale(HID)
    col = 0.6 + 0.6 * np.random.standard_normal(Y_DIM)
    return {
        "x_samples": bf(np.random.standard_normal((N, X_DIM)) * s),
        "y_samples": bf(np.random.standard_normal((N, Y_DIM)) + col),
        "mu_W1": bf(np.random.standard_normal((X_DIM, HID)) / np.sqrt(X_DIM) / s[:, None] * t),
        "mu_b1": bf(np.random.standard_normal(HID) * 0.8 * t),
        "mu_W2": bf(np.random.standard_normal((HID, Y_DIM)) * 1.2 / np.sqrt(HID) / t[:, None]),
        "mu_b2": bf(0.4 + 0.4 * np.random.standard_normal(Y_DIM)),
        "lv_W1": bf(np.random.standard_normal((X_DIM, HID)) / np.sqrt(X_DIM) / s[:, None] * u),
        "lv_b1": bf(np.random.standard_normal(HID) * 0.8 * u),
        "lv_W2": bf(np.random.standard_normal((HID, Y_DIM)) / np.sqrt(HID) / u[:, None]),
        "lv_b2": bf(0.3 + 0.4 * np.random.standard_normal(Y_DIM)),
    }


def reference(x_samples, y_samples, mu_W1, mu_b1, mu_W2, mu_b2, lv_W1, lv_b1, lv_W2, lv_b2):
    x = f64(x_samples)
    y = f64(y_samples)
    xq = mxq(x, 1, "e4m3")
    h_mu = np.maximum((xq @ mxq(f64(mu_W1), 0, "e4m3")) + f64(mu_b1), 0.0)
    mu = (mxq(h_mu, 1, "e4m3") @ mxq(f64(mu_W2), 0, "e4m3")) + f64(mu_b2)
    h_lv = np.maximum((xq @ mxq(f64(lv_W1), 0, "e4m3")) + f64(lv_b1), 0.0)
    logvar = np.tanh((mxq(h_lv, 1, "e4m3") @ mxq(f64(lv_W2), 0, "e4m3")) + f64(lv_b2))
    w = 0.5 * np.exp(-logvar)
    n = x.shape[0]
    pos_row = -(((mu - y) ** 2) * w).sum(axis=1)
    Sy = y.sum(axis=0)
    Sy2 = (y ** 2).sum(axis=0)
    neg_row = -(w * (n * mu ** 2 - 2.0 * mu * Sy + Sy2)).sum(axis=1) / (n * n)
    return pos_row, neg_row

@@ -1,0 +1,393 @@
+from contextlib import ExitStack
+
+import concourse.mybir as mybir
+from concourse.masks import make_identity
+
+F32 = mybir.dt.float32
+BF16 = mybir.dt.bfloat16
+U32 = mybir.dt.uint32
+U8 = mybir.dt.uint8
+FP8X4 = mybir.dt.float8_e4m3fn_x4
+ACT = mybir.ActivationFunctionType
+ALU = mybir.AluOpType
+AX = mybir.AxisListType
+
+P = 128
+N_S = 4096
+X_DIM = 512
+HID = 1024
+Y_DIM = 128
+CH = 512
+N_CH = N_S // CH
+N_UNITS = 4 * N_CH
+JT = N_S // P
+Y_PITCH = 144
+
+FLOPS = 2 * N_S * (2 * X_DIM * HID + 2 * HID * Y_DIM)
+
+MANUAL = True
+
+
+def tile_infoncemi_pa_t_kernel(
+    tc, x_samples, y_samples, mu_W1, mu_b1, mu_W2, mu_b2, lv_W1, lv_b1, lv_W2, lv_b2, out_0, out_1
+):
+    nc = tc.nc
+    w1_dram = (lv_W1, mu_W1)
+    b1_dram = (lv_b1, mu_b1)
+    w2_dram = (lv_W2, mu_W2)
+    b2_dram = (lv_b2, mu_b2)
+    inv_n = 1.0 / N_S
+
+    with ExitStack() as ctx:
+        keep = ctx.enter_context(tc.tile_pool(name="keep", bufs=1))
+        work = ctx.enter_context(tc.tile_pool(name="work", bufs=2))
+        psum = ctx.enter_context(tc.psum_pool(name="psum", bufs=1))
+        if MANUAL:
+            ctx.enter_context(tc.manual_schedule())
+
+        x_sb = keep.tile([P, JT * X_DIM], BF16)
+        xc = keep.tile([P, N_S], U32, align_bytes=64)
+        xs = keep.tile([P, N_S], U8, align_bytes=64)
+        w1raw = [keep.tile([P, 4, HID], BF16, name="w1raw%d" % h) for h in range(2)]
+        w1c = [keep.tile([P, HID], U32, name="w1c%d" % h, align_bytes=64) for h in range(2)]
+        w1s = [keep.tile([P, HID], U8, name="w1s%d" % h, align_bytes=64) for h in range(2)]
+        w2raw = [keep.tile([P, 8, Y_DIM], BF16, name="w2raw%d" % h) for h in range(2)]
+        w2c = [keep.tile([P, 2 * Y_DIM], U32, name="w2c%d" % h, align_bytes=64) for h in range(2)]
+        w2s = [keep.tile([P, 2 * Y_DIM], U8, name="w2s%d" % h, align_bytes=64) for h in range(2)]
+        y_sb = keep.tile([P, JT, Y_PITCH], BF16)
+        yT = keep.tile([P, N_S], BF16)
+        braw = keep.tile([P, P], BF16)
+        bias_sb = keep.tile([P, 32], F32)
+        ident_f = keep.tile([P, P], F32)
+        ident_b = keep.tile([P, P], BF16)
+        cred = keep.tile([P, 2], F32)
+        stat = keep.tile([P, 8], F32)
+        r_sb = keep.tile([P, 2, JT], F32)
+
+        nc.vector.memset(braw[:], 0.0)
+        for h in range(2):
+            nc.scalar.dma_start(out=braw[8 * h : 8 * h + 8, :], in_=b1_dram[h].rearrange("(m p) -> m p", p=P))
+        for h in range(2):
+            nc.scalar.dma_start(out=braw[16 + h : 17 + h, :], in_=b2_dram[h].rearrange("(o p) -> o p", o=1))
+
+        x_rows = x_samples.rearrange("(p j) k -> p (j k)", j=JT)
+
+        def load_x(c):
+            cols = slice(4 * X_DIM * c, 4 * X_DIM * (c + 1))
+            nc.sync.dma_start(out=x_sb[:, cols], in_=x_rows[:, cols])
+
+        def load_w1(h, g):
+            cols = slice(512 * g, 512 * (g + 1))
+            for u in range(2):
+                nc.sync.dma_start(
+                    out=w1raw[h][:, 2 * u : 2 * u + 2, cols],
+                    in_=w1_dram[h][256 * u : 256 * (u + 1), cols].rearrange("(q e) c -> q e c", e=2),
+                )
+
+        load_x(0)
+        load_w1(0, 0)
+        load_w1(0, 1)
+        nc.vector.memset(y_sb[:, :, Y_DIM:Y_PITCH], 1.0)
+        nc.sync.dma_start(out=y_sb[:, :, 0:Y_DIM], in_=y_samples.rearrange("(p j) d -> p j d", j=JT))
+        load_w1(1, 0)
+        load_w1(1, 1)
+        nc.sync.dma_start(out=w2raw[0][:], in_=w2_dram[0].rearrange("(m p) n -> p m n", p=P))
+        load_x(1)
+        nc.sync.dma_start(out=w2raw[1][:], in_=w2_dram[1].rearrange("(m p) n -> p m n", p=P))
+        for c in range(2, N_CH):
+            load_x(c)
+
+        make_identity(nc, ident_b[:])
+        make_identity(nc, ident_f[:])
+        nc.vector.memset(cred[:, 0:1], -0.5)
+        nc.vector.memset(cred[:, 1:2], -0.5 * inv_n)
+
+        x_words = x_sb[:].bitcast(F32)
+
+        def x_transposes(c, half, tag):
+            xt = psum.tile([P, 512], F32, tag=tag, name="xt")
+            for jj in range(2):
+                j = 4 * c + 2 * half + jj
+                for u in range(2):
+                    nc.tensor.transpose(
+                        xt[:, 128 * (2 * jj + u) : 128 * (2 * jj + u + 1)],
+                        x_words[:, 256 * j + 128 * u : 256 * j + 128 * (u + 1)],
+                        ident_f[:],
+                    )
+            return xt
+
+        def x_evac(xg, half, xt):
+            dst = xg[:].rearrange("q (j s u) -> q j s u", j=4, s=P, u=2)[:, 2 * half : 2 * half + 2]
+            nc.scalar.copy(out=dst, in_=xt[:].rearrange("q (j u s) -> q j s u", j=2, u=2, s=P))
+
+        def x_quant(c, xg):
+            cols = slice(CH * c, CH * (c + 1))
+            nc.vector.quantize_mx(out=xc[:, cols].bitcast(FP8X4), scales=xs[:, cols], in_=xg[:].bitcast(BF16))
+
+        def w1_regroup(h, g):
+            wg = work.tile([P, 512, 4], BF16, tag="wg", name="wg", align_bytes=64)
+            nc.vector.tensor_copy(
+                out=wg[:].rearrange("p (c i) t -> p c t i", i=4),
+                in_=w1raw[h][:, :, 512 * g : 512 * (g + 1)].rearrange("p t (c i) -> p c t i", i=4),
+            )
+            return wg
+
+        def w1_quant(h, g, wg):
+            cols = slice(512 * g, 512 * (g + 1))
+            nc.vector.quantize_mx(
+                out=w1c[h][:, cols].bitcast(FP8X4), scales=w1s[h][:, cols], in_=wg[:].rearrange("p c t -> p (c t)")
+            )
+
+        def w2_regroup(h):
+            w2g = work.tile([P, 2, Y_DIM, 4], BF16, tag="w2g", name="w2g", align_bytes=64)
+            nc.vector.tensor_copy(out=w2g[:], in_=w2raw[h][:].rearrange("p (g t) n -> p g n t", t=4))
+            return w2g
+
+        def w2_quant(h, w2g):
+            nc.vector.quantize_mx(
+                out=w2c[h][:].bitcast(FP8X4), scales=w2s[h][:], in_=w2g[:].rearrange("p g n t -> p (g n t)")
+            )
+
+        bt_ps = psum.tile([P, P], BF16, tag="m0", name="bt_ps")
+        nc.tensor.transpose(bt_ps[:], braw[:], ident_b[:])
+        nc.vector.tensor_copy(out=bias_sb[:], in_=bt_ps[:, 0:32])
+
+        xg_tiles = {}
+        xg_tiles[0] = work.tile([P, 2 * CH], F32, tag="xg", name="xg", align_bytes=64)
+        xt_a = x_transposes(0, 0, "s1_0")
+        xt_b = x_transposes(0, 1, "s1_1")
+        x_evac(xg_tiles[0], 0, xt_a)
+        x_evac(xg_tiles[0], 1, xt_b)
+        wg0 = w1_regroup(0, 0)
+        x_quant(0, xg_tiles[0])
+        w1_quant(0, 0, wg0)
+
+        banks = {}
+        hc = {}
+        hg = {}
+        hq = {}
+        hs = {}
+        acc = {}
+        ep = {}
+        misc = {}
+
+        def unit(n):
+            c, k = divmod(n, 4)
+            return c, k // 2, k % 2
+
+        def stage1(n, t):
+            c, h, g = unit(n)
+            bank = psum.tile([P, CH], F32, tag="s1_%d" % t, name="bank")
+            banks[(n, t)] = bank
+            wcols = slice(512 * g + 128 * t, 512 * g + 128 * (t + 1))
+            xcols = slice(CH * c, CH * (c + 1))
+            nc.tensor.matmul_mx(
+                out=bank[:],
+                lhsT=w1c[h][:, wcols].bitcast(FP8X4),
+                lhsT_scale=w1s[h][:, wcols],
+                rhs=xc[:, xcols].bitcast(FP8X4),
+                rhs_scale=xs[:, xcols],
+                start=True,
+                stop=True,
+            )
+
+        def evac(n, t, on_vector):
+            c, h, g = unit(n)
+            if t == 0:
+                hc[n] = work.tile([P, 4, CH], BF16, tag="hc", name="hc")
+            col = 8 * h + 4 * g + t
+            bank = banks[(n, t)]
+            if on_vector:
+                nc.vector.tensor_scalar(
+                    out=hc[n][:, t, :], in0=bank[:], scalar1=bias_sb[:, col : col + 1], scalar2=0.0,
+                    op0=ALU.add, op1=ALU.max,
+                )
+            else:
+                nc.scalar.activation(out=hc[n][:, t, :], in_=bank[:], func=ACT.Relu, bias=bias_sb[:, col : col + 1])
+
+        def regroup(n):
+            hg[n] = work.tile([P, CH, 4], BF16, tag="hg", name="hg", align_bytes=64)
+            nc.vector.tensor_copy(
+                out=hg[n][:].rearrange("p (c i) t -> p c t i", i=4),
+                in_=hc[n][:].rearrange("p t (c i) -> p c t i", i=4),
+            )
+
+        def quant(n):
+            hq[n] = work.tile([P, CH], U32, tag="hq", name="hq", align_bytes=64)
+            hs[n] = work.tile([P, CH], U8, tag="hs", name="hs", align_bytes=64)
+            nc.vector.quantize_mx(
+                out=hq[n][:].bitcast(FP8X4), scales=hs[n][:], in_=hg[n][:].rearrange("p c t -> p (c t)")
+            )
+
+        def stage2(n):
+            c, h, g = unit(n)
+            if g == 0:
+                acc[(c, h)] = psum.tile([P, CH], F32, tag="acc%d" % h, name="acc")
+            cols = slice(Y_DIM * g, Y_DIM * (g + 1))
+            nc.tensor.matmul_mx(
+                out=acc[(c, h)][:],
+                lhsT=w2c[h][:, cols].bitcast(FP8X4),
+                lhsT_scale=w2s[h][:, cols],
+                rhs=hq[n][:].bitcast(FP8X4),
+                rhs_scale=hs[n][:],
+                start=(g == 0),
+                stop=(g == 1),
+            )
+
+        def ep_tile(c, what):
+            ep[(c, what)] = work.tile([P, CH], F32, tag="ep_" + what, name="ep_" + what)
+            return ep[(c, what)]
+
+        def tanh_lv(c):
+            nc.scalar.activation(out=ep_tile(c, "th")[:], in_=acc[(c, 0)][:], func=ACT.Tanh, bias=bias_sb[:, 16:17])
+
+        def exp_w(c):
+            nc.scalar.activation(out=ep_tile(c, "w")[:], in_=ep[(c, "th")][:], func=ACT.Exp, scale=-1.0)
+
+        def sq_e(c):
+            nc.scalar.activation(out=ep_tile(c, "e2")[:], in_=acc[(c, 1)][:], func=ACT.Square, bias=stat[:, 2:3])
+
+        def diff_d(c):
+            nc.vector.scalar_tensor_tensor(
+                out=ep_tile(c, "d")[:], in0=acc[(c, 1)][:], scalar=bias_sb[:, 17:18],
+                in1=yT[:, CH * c : CH * (c + 1)], op0=ALU.add, op1=ALU.subtract,
+            )
+
+        def sq_d(c):
+            nc.scalar.activation(out=ep_tile(c, "d2")[:], in_=ep[(c, "d")][:], func=ACT.Square)
+
+        def term_q(c):
+            nc.vector.scalar_tensor_tensor(
+                out=ep_tile(c, "q")[:], in0=ep[(c, "e2")][:], scalar=stat[:, 4:5], in1=ep[(c, "w")][:],
+                op0=ALU.add, op1=ALU.mult,
+            )
+
+        def term_p(c):
+            nc.vector.tensor_tensor(out=ep_tile(c, "p")[:], in0=ep[(c, "d2")][:], in1=ep[(c, "w")][:], op=ALU.mult)
+
+        def sums_over_d(c, what):
+            o = 0 if what == "p" else 1
+            if what == "q":
+                misc["r"] = psum.tile([P, 8], F32, tag="m0", name="r_ps")
+            term = ep[(c, what)]
+            for j in range(4):
+                nc.tensor.matmul(
+                    out=misc["r"][:, 4 * o + j : 4 * o + j + 1], lhsT=term[:, P * j : P * (j + 1)],
+                    rhs=cred[:, o : o + 1], start=True, stop=True,
+                )
+
+        def keep_sums(c):
+            nc.vector.tensor_copy(
+                out=r_sb[:, :, 4 * c : 4 * (c + 1)], in_=misc["r"][:].rearrange("p (o j) -> p o j", o=2)
+            )
+
+        for s in range(N_UNITS):
+            c, r = divmod(s, 4)
+            ce = c - 1
+            cf = c - 2
+            cn = c + 1
+            last = s == N_UNITS - 1
+
+            stage1(s, 0)
+            if s >= 3:
+                stage2(s - 3)
+            for t in range(1, 4):
+                stage1(s, t)
+            if cf >= 0 and r == 0:
+                sums_over_d(cf, "q")
+            if cf >= 0 and r == 1:
+                sums_over_d(cf, "p")
+            if cn < N_CH and r == 1:
+                misc["xa"] = x_transposes(cn, 0, "m1")
+            if cn < N_CH and r == 2:
+                misc["xb"] = x_transposes(cn, 1, "m0")
+            if s < 4:
+                yt = psum.tile([P, 8 * P], BF16, tag=("m0", "m0", "m1", "m1")[s], name="yt")
+                if s == 0:
+                    g_ps = psum.tile([P, 256], F32, tag="acc1", name="g_ps")
+                for i in range(8):
+                    nc.tensor.transpose(yt[:, P * i : P * (i + 1)], y_sb[:, 8 * s + i, 0:Y_DIM], ident_b[:])
+                for i in range(8):
+                    j = 8 * s + i
+                    nc.tensor.matmul(
+                        out=g_ps[:, 0 : Y_DIM + 2], lhsT=y_sb[:, j, 0:Y_DIM], rhs=y_sb[:, j, 0 : Y_DIM + 2],
+                        start=(j == 0), stop=(j == JT - 1),
+                    )
+
+            wnext = {0: (0, 1), 1: (1, 0), 2: (1, 1)}.get(s)
+            if wnext is not None:
+                wg = w1_regroup(wnext[0], wnext[1])
+            if s in (2, 3):
+                w2g = w2_regroup(s - 2)
+            if s >= 1:
+                regroup(s - 1)
+            if wnext is not None:
+                w1_quant(wnext[0], wnext[1], wg)
+            if s in (2, 3):
+                w2_quant(s - 2, w2g)
+            if s >= 2:
+                quant(s - 2)
+            if s == 4:
+                gd = work.tile([P, P], F32, tag="gd", name="gd")
+                nc.vector.tensor_tensor(out=gd[:], in0=g_ps[:, 0:P], in1=ident_f[:], op=ALU.mult)
+                nc.vector.reduce_sum(out=stat[:, 0:1], in_=gd[:], axis=AX.X)
+                nc.vector.tensor_scalar(
+                    out=stat[:, 1:2], in0=g_ps[:, P : P + 1], scalar1=inv_n, scalar2=None, op0=ALU.mult
+                )
+                nc.vector.tensor_tensor(out=stat[:, 2:3], in0=bias_sb[:, 17:18], in1=stat[:, 1:2], op=ALU.subtract)
+                nc.vector.tensor_tensor(out=stat[:, 3:4], in0=stat[:, 1:2], in1=stat[:, 1:2], op=ALU.mult)
+                nc.vector.scalar_tensor_tensor(
+                    out=stat[:, 4:5], in0=stat[:, 0:1], scalar=inv_n, in1=stat[:, 3:4], op0=ALU.mult, op1=ALU.subtract
+                )
+
+            if ce >= 0:
+                (tanh_lv, exp_w, sq_e, sq_d)[r](ce)
+            v_bank = c >= 1 and (r < 3 or last)
+            for t in range(3 if v_bank else 4):
+                evac(s, t, False)
+            if cn < N_CH and r == 1:
+                xg_tiles[cn] = work.tile([P, 2 * CH], F32, tag="xg", name="xg", align_bytes=64)
+                x_evac(xg_tiles[cn], 0, misc["xa"])
+            if cn < N_CH and r == 2:
+                x_evac(xg_tiles[cn], 1, misc["xb"])
+            if s < 4:
+                nc.scalar.copy(out=yT[:, 8 * P * s : 8 * P * (s + 1)], in_=yt[:])
+
+            if cn < N_CH and r == 3:
+                x_quant(cn, xg_tiles[cn])
+            if ce >= 0 and r == 2:
+                diff_d(ce)
+            if ce >= 0 and r == 3 and not last:
+                term_q(ce)
+            if cf >= 0 and r == 0:
+                term_p(cf)
+            if v_bank:
+                evac(s, 3, True)
+            if cf >= 0 and r == 1:
+                keep_sums(cf)
+
+        lc = N_CH - 1
+        stage2(N_UNITS - 3)
+        regroup(N_UNITS - 1)
+        quant(N_UNITS - 2)
+        quant(N_UNITS - 1)
+        tanh_lv(lc)
+        exp_w(lc)
+        stage2(N_UNITS - 2)
+        stage2(N_UNITS - 1)
+        term_q(lc - 1)
+        term_p(lc - 1)
+        sums_over_d(lc - 1, "q")
+        sums_over_d(lc - 1, "p")
+        keep_sums(lc - 1)
+        sq_e(lc)
+        diff_d(lc)
+        sq_d(lc)
+        term_q(lc)
+        term_p(lc)
+        sums_over_d(lc, "q")
+        sums_over_d(lc, "p")
+        keep_sums(lc)
+
+        nc.sync.dma_start(out=out_0.rearrange("(p j) -> p j", j=JT), in_=r_sb[:, 0, :])
+        nc.scalar.dma_start(out=out_1.rearrange("(p j) -> p j", j=JT), in_=r_sb[:, 1, :])

@@ -26,6 +26,11 @@ Y_PITCH = 144
 FLOPS = 2 * N_S * (2 * X_DIM * HID + 2 * HID * Y_DIM)
 
 MANUAL = True
+LAG_C = 2
+LAG_D = 3
+LAG_E = 4
+V_STEPS = 3
+GRAM_0 = 2
 
 
 def tile_infoncemi_pa_t_kernel(
@@ -62,18 +67,12 @@ def tile_infoncemi_pa_t_kernel(
         ident_b = keep.tile([P, P], BF16)
         cred = keep.tile([P, 2], F32)
         stat = keep.tile([P, 8], F32)
-        r_sb = keep.tile([P, 2, JT], F32)
-
-        nc.vector.memset(braw[:], 0.0)
-        for h in range(2):
-            nc.scalar.dma_start(out=braw[8 * h : 8 * h + 8, :], in_=b1_dram[h].rearrange("(m p) -> m p", p=P))
-        for h in range(2):
-            nc.scalar.dma_start(out=braw[16 + h : 17 + h, :], in_=b2_dram[h].rearrange("(o p) -> o p", o=1))
+        r_sb = keep.tile([P, 2 * JT], F32)
 
         x_rows = x_samples.rearrange("(p j) k -> p (j k)", j=JT)
 
-        def load_x(c):
-            cols = slice(4 * X_DIM * c, 4 * X_DIM * (c + 1))
+        def load_x(first_tile, n_tiles):
+            cols = slice(X_DIM * first_tile, X_DIM * (first_tile + n_tiles))
             nc.sync.dma_start(out=x_sb[:, cols], in_=x_rows[:, cols])
 
         def load_w1(h, g):
@@ -84,21 +83,27 @@ def tile_infoncemi_pa_t_kernel(
                     in_=w1_dram[h][256 * u : 256 * (u + 1), cols].rearrange("(q e) c -> q e c", e=2),
                 )
 
-        load_x(0)
+        load_x(0, 2)
+        load_x(2, 2)
+        nc.vector.memset(braw[:], 0.0)
+        for h in range(2):
+            nc.scalar.dma_start(out=braw[8 * h : 8 * h + 8, :], in_=b1_dram[h].rearrange("(m p) -> m p", p=P))
+        for h in range(2):
+            nc.scalar.dma_start(out=braw[16 + h : 17 + h, :], in_=b2_dram[h].rearrange("(o p) -> o p", o=1))
         load_w1(0, 0)
         load_w1(0, 1)
-        nc.vector.memset(y_sb[:, :, Y_DIM:Y_PITCH], 1.0)
-        nc.sync.dma_start(out=y_sb[:, :, 0:Y_DIM], in_=y_samples.rearrange("(p j) d -> p j d", j=JT))
+        load_x(4, 4)
         load_w1(1, 0)
         load_w1(1, 1)
-        nc.sync.dma_start(out=w2raw[0][:], in_=w2_dram[0].rearrange("(m p) n -> p m n", p=P))
-        load_x(1)
-        nc.sync.dma_start(out=w2raw[1][:], in_=w2_dram[1].rearrange("(m p) n -> p m n", p=P))
+        nc.vector.memset(y_sb[:, :, Y_DIM:Y_PITCH], 1.0)
+        nc.sync.dma_start(out=y_sb[:, :, 0:Y_DIM], in_=y_samples.rearrange("(p j) d -> p j d", j=JT))
+        for h in range(2):
+            nc.sync.dma_start(out=w2raw[h][:], in_=w2_dram[h].rearrange("(m p) n -> p m n", p=P))
         for c in range(2, N_CH):
-            load_x(c)
+            load_x(4 * c, 4)
 
-        make_identity(nc, ident_b[:])
         make_identity(nc, ident_f[:])
+        make_identity(nc, ident_b[:])
         nc.vector.memset(cred[:, 0:1], -0.5)
         nc.vector.memset(cred[:, 1:2], -0.5 * inv_n)
 
@@ -148,19 +153,16 @@ def tile_infoncemi_pa_t_kernel(
                 out=w2c[h][:].bitcast(FP8X4), scales=w2s[h][:], in_=w2g[:].rearrange("p g n t -> p (g n t)")
             )
 
-        bt_ps = psum.tile([P, P], BF16, tag="m0", name="bt_ps")
-        nc.tensor.transpose(bt_ps[:], braw[:], ident_b[:])
-        nc.vector.tensor_copy(out=bias_sb[:], in_=bt_ps[:, 0:32])
-
         xg_tiles = {}
         xg_tiles[0] = work.tile([P, 2 * CH], F32, tag="xg", name="xg", align_bytes=64)
-        xt_a = x_transposes(0, 0, "s1_0")
-        xt_b = x_transposes(0, 1, "s1_1")
-        x_evac(xg_tiles[0], 0, xt_a)
-        x_evac(xg_tiles[0], 1, xt_b)
+        for half in range(2):
+            x_evac(xg_tiles[0], half, x_transposes(0, half, "s1_%d" % half))
+        bt_ps = psum.tile([P, P], BF16, tag="mx", name="bt_ps")
+        nc.tensor.transpose(bt_ps[:], braw[:], ident_b[:])
         wg0 = w1_regroup(0, 0)
-        x_quant(0, xg_tiles[0])
+        nc.vector.tensor_copy(out=bias_sb[:], in_=bt_ps[:, 0:32])
         w1_quant(0, 0, wg0)
+        x_quant(0, xg_tiles[0])
 
         banks = {}
         hc = {}
@@ -194,7 +196,7 @@ def tile_infoncemi_pa_t_kernel(
         def evac(n, t, on_vector):
             c, h, g = unit(n)
             if t == 0:
-                hc[n] = work.tile([P, 4, CH], BF16, tag="hc", name="hc")
+                hc[n] = work.tile([P, 4, CH], BF16, tag="hc", name="hc", bufs=LAG_C + 2)
             col = 8 * h + 4 * g + t
             bank = banks[(n, t)]
             if on_vector:
@@ -213,8 +215,8 @@ def tile_infoncemi_pa_t_kernel(
             )
 
         def quant(n):
-            hq[n] = work.tile([P, CH], U32, tag="hq", name="hq", align_bytes=64)
-            hs[n] = work.tile([P, CH], U8, tag="hs", name="hs", align_bytes=64)
+            hq[n] = work.tile([P, CH], U32, tag="hq", name="hq", align_bytes=64, bufs=3)
+            hs[n] = work.tile([P, CH], U8, tag="hs", name="hs", align_bytes=64, bufs=3)
             nc.vector.quantize_mx(
                 out=hq[n][:].bitcast(FP8X4), scales=hs[n][:], in_=hg[n][:].rearrange("p c t -> p (c t)")
             )
@@ -256,6 +258,9 @@ def tile_infoncemi_pa_t_kernel(
         def sq_d(c):
             nc.scalar.activation(out=ep_tile(c, "d2")[:], in_=ep[(c, "d")][:], func=ACT.Square)
 
+        def sq_d_on_vector(c):
+            nc.vector.tensor_tensor(out=ep_tile(c, "d2")[:], in0=ep[(c, "d")][:], in1=ep[(c, "d")][:], op=ALU.mult)
+
         def term_q(c):
             nc.vector.scalar_tensor_tensor(
                 out=ep_tile(c, "q")[:], in0=ep[(c, "e2")][:], scalar=stat[:, 4:5], in1=ep[(c, "w")][:],
@@ -267,67 +272,78 @@ def tile_infoncemi_pa_t_kernel(
 
         def sums_over_d(c, what):
             o = 0 if what == "p" else 1
-            if what == "q":
-                misc["r"] = psum.tile([P, 8], F32, tag="m0", name="r_ps")
             term = ep[(c, what)]
             for j in range(4):
+                col = JT * o + 4 * c + j
                 nc.tensor.matmul(
-                    out=misc["r"][:, 4 * o + j : 4 * o + j + 1], lhsT=term[:, P * j : P * (j + 1)],
-                    rhs=cred[:, o : o + 1], start=True, stop=True,
+                    out=misc["r"][:, col : col + 1], lhsT=term[:, P * j : P * (j + 1)], rhs=cred[:, o : o + 1],
+                    start=True, stop=True,
                 )
 
-        def keep_sums(c):
-            nc.vector.tensor_copy(
-                out=r_sb[:, :, 4 * c : 4 * (c + 1)], in_=misc["r"][:].rearrange("p (o j) -> p o j", o=2)
-            )
+        def sums_q(c):
+            sums_over_d(c, "q")
 
-        for s in range(N_UNITS):
+        def sums_p(c):
+            sums_over_d(c, "p")
+
+        def run_due(s, table):
+            for offset, op in table:
+                k, rem = divmod(s - offset, 4)
+                if rem == 0 and 0 <= k < N_CH - 1:
+                    op(k)
+
+        last = N_CH - 1
+        for s in range(N_UNITS + LAG_E):
             c, r = divmod(s, 4)
-            ce = c - 1
-            cf = c - 2
+            live = s < N_UNITS
             cn = c + 1
-            last = s == N_UNITS - 1
 
-            stage1(s, 0)
-            if s >= 3:
-                stage2(s - 3)
-            for t in range(1, 4):
-                stage1(s, t)
-            if cf >= 0 and r == 0:
-                sums_over_d(cf, "q")
-            if cf >= 0 and r == 1:
-                sums_over_d(cf, "p")
-            if cn < N_CH and r == 1:
-                misc["xa"] = x_transposes(cn, 0, "m1")
-            if cn < N_CH and r == 2:
-                misc["xb"] = x_transposes(cn, 1, "m0")
-            if s < 4:
-                yt = psum.tile([P, 8 * P], BF16, tag=("m0", "m0", "m1", "m1")[s], name="yt")
-                if s == 0:
-                    g_ps = psum.tile([P, 256], F32, tag="acc1", name="g_ps")
+            if live:
+                stage1(s, 0)
+            if s >= LAG_E:
+                stage2(s - LAG_E)
+            if live:
+                for t in range(1, 4):
+                    stage1(s, t)
+            if s == LAG_E + 6:
+                misc["r"] = psum.tile([P, 2 * JT], F32, tag="mr", name="r_ps")
+            run_due(s, ((LAG_E + 6, sums_q), (LAG_E + 7, sums_p)))
+            x_fill = live and cn < N_CH and r < 2
+            y_fill = live and r == 2 and c % 2 == 0
+            if x_fill:
+                fill = x_transposes(cn, r, "mx")
+            if y_fill:
+                fill = psum.tile([P, 8 * P], BF16, tag="mx", name="yt")
                 for i in range(8):
-                    nc.tensor.transpose(yt[:, P * i : P * (i + 1)], y_sb[:, 8 * s + i, 0:Y_DIM], ident_b[:])
+                    nc.tensor.transpose(fill[:, P * i : P * (i + 1)], y_sb[:, 4 * c + i, 0:Y_DIM], ident_b[:])
+            if GRAM_0 <= s < GRAM_0 + 4:
+                if s == GRAM_0:
+                    g_ps = psum.tile([P, 256], F32, tag="mr", name="g_ps")
                 for i in range(8):
-                    j = 8 * s + i
+                    j = 8 * (s - GRAM_0) + i
                     nc.tensor.matmul(
                         out=g_ps[:, 0 : Y_DIM + 2], lhsT=y_sb[:, j, 0:Y_DIM], rhs=y_sb[:, j, 0 : Y_DIM + 2],
                         start=(j == 0), stop=(j == JT - 1),
                     )
 
+            if live:
+                run_due(s, ((LAG_E + 4, diff_d),))
             wnext = {0: (0, 1), 1: (1, 0), 2: (1, 1)}.get(s)
             if wnext is not None:
                 wg = w1_regroup(wnext[0], wnext[1])
             if s in (2, 3):
                 w2g = w2_regroup(s - 2)
-            if s >= 1:
-                regroup(s - 1)
+            if 0 <= s - LAG_D < N_UNITS:
+                quant(s - LAG_D)
             if wnext is not None:
                 w1_quant(wnext[0], wnext[1], wg)
             if s in (2, 3):
                 w2_quant(s - 2, w2g)
-            if s >= 2:
-                quant(s - 2)
-            if s == 4:
+            if 0 <= s - LAG_C < N_UNITS:
+                regroup(s - LAG_C)
+            if not live:
+                run_due(s, ((LAG_E + 4, diff_d),))
+            if s == GRAM_0 + 5:
                 gd = work.tile([P, P], F32, tag="gd", name="gd")
                 nc.vector.tensor_tensor(out=gd[:], in0=g_ps[:, 0:P], in1=ident_f[:], op=ALU.mult)
                 nc.vector.reduce_sum(out=stat[:, 0:1], in_=gd[:], axis=AX.X)
@@ -340,54 +356,36 @@ def tile_infoncemi_pa_t_kernel(
                     out=stat[:, 4:5], in0=stat[:, 0:1], scalar=inv_n, in1=stat[:, 3:4], op0=ALU.mult, op1=ALU.subtract
                 )
 
-            if ce >= 0:
-                (tanh_lv, exp_w, sq_e, sq_d)[r](ce)
-            v_bank = c >= 1 and (r < 3 or last)
-            for t in range(3 if v_bank else 4):
-                evac(s, t, False)
-            if cn < N_CH and r == 1:
-                xg_tiles[cn] = work.tile([P, 2 * CH], F32, tag="xg", name="xg", align_bytes=64)
-                x_evac(xg_tiles[cn], 0, misc["xa"])
-            if cn < N_CH and r == 2:
-                x_evac(xg_tiles[cn], 1, misc["xb"])
-            if s < 4:
-                nc.scalar.copy(out=yT[:, 8 * P * s : 8 * P * (s + 1)], in_=yt[:])
+            v_bank = live and c >= 1 and r < V_STEPS
+            if live:
+                for t in range(3 if v_bank else 4):
+                    evac(s, t, False)
+            run_due(s, ((LAG_E + 2, tanh_lv), (LAG_E + 3, exp_w), (LAG_E + 4, sq_e), (LAG_E + 5, sq_d)))
+            if s == 4 * last + LAG_E + 2:
+                tanh_lv(last)
+            if s == 4 * last + LAG_E + 3:
+                exp_w(last)
+            if x_fill:
+                if r == 0:
+                    xg_tiles[cn] = work.tile([P, 2 * CH], F32, tag="xg", name="xg", align_bytes=64)
+                x_evac(xg_tiles[cn], r, fill)
+            if y_fill:
+                nc.scalar.copy(out=yT[:, CH * c : CH * (c + 2)], in_=fill[:])
 
-            if cn < N_CH and r == 3:
+            run_due(s, ((LAG_E + 5, term_q), (LAG_E + 6, term_p)))
+            if live and cn < N_CH and r == 2:
                 x_quant(cn, xg_tiles[cn])
-            if ce >= 0 and r == 2:
-                diff_d(ce)
-            if ce >= 0 and r == 3 and not last:
-                term_q(ce)
-            if cf >= 0 and r == 0:
-                term_p(cf)
             if v_bank:
                 evac(s, 3, True)
-            if cf >= 0 and r == 1:
-                keep_sums(cf)
 
-        lc = N_CH - 1
-        stage2(N_UNITS - 3)
-        regroup(N_UNITS - 1)
-        quant(N_UNITS - 2)
-        quant(N_UNITS - 1)
-        tanh_lv(lc)
-        exp_w(lc)
-        stage2(N_UNITS - 2)
-        stage2(N_UNITS - 1)
-        term_q(lc - 1)
-        term_p(lc - 1)
-        sums_over_d(lc - 1, "q")
-        sums_over_d(lc - 1, "p")
-        keep_sums(lc - 1)
-        sq_e(lc)
-        diff_d(lc)
-        sq_d(lc)
-        term_q(lc)
-        term_p(lc)
-        sums_over_d(lc, "q")
-        sums_over_d(lc, "p")
-        keep_sums(lc)
+        diff_d(last)
+        sq_e(last)
+        sq_d_on_vector(last)
+        term_p(last)
+        sums_p(last)
+        term_q(last)
+        sums_q(last)
 
-        nc.sync.dma_start(out=out_0.rearrange("(p j) -> p j", j=JT), in_=r_sb[:, 0, :])
-        nc.scalar.dma_start(out=out_1.rearrange("(p j) -> p j", j=JT), in_=r_sb[:, 1, :])
+        nc.vector.tensor_copy(out=r_sb[:], in_=misc["r"][:])
+        nc.sync.dma_start(out=out_0.rearrange("(p j) -> p j", j=JT), in_=r_sb[:, 0:JT])
+        nc.scalar.dma_start(out=out_1.rearrange("(p j) -> p j", j=JT), in_=r_sb[:, JT : 2 * JT])

@@ -68,6 +68,7 @@ def tile_infoncemi_pa_t_kernel(
         cred = keep.tile([P, 2], F32)
         stat = keep.tile([P, 8], F32)
         r_sb = keep.tile([P, 2 * JT], F32)
+        warm = keep.tile([P, 1], F32)
 
         x_rows = x_samples.rearrange("(p j) k -> p (j k)", j=JT)
 
@@ -106,6 +107,7 @@ def tile_infoncemi_pa_t_kernel(
         make_identity(nc, ident_b[:])
         nc.vector.memset(cred[:, 0:1], -0.5)
         nc.vector.memset(cred[:, 1:2], -0.5 * inv_n)
+        nc.scalar.activation(out=warm[:], in_=cred[:, 0:1], func=ACT.Exp)
 
         x_words = x_sb[:].bitcast(F32)
 
@@ -388,4 +390,4 @@ def tile_infoncemi_pa_t_kernel(
 
         nc.vector.tensor_copy(out=r_sb[:], in_=misc["r"][:])
         nc.sync.dma_start(out=out_0.rearrange("(p j) -> p j", j=JT), in_=r_sb[:, 0:JT])
-        nc.scalar.dma_start(out=out_1.rearrange("(p j) -> p j", j=JT), in_=r_sb[:, JT : 2 * JT])
+        nc.sync.dma_start(out=out_1.rearrange("(p j) -> p j", j=JT), in_=r_sb[:, JT : 2 * JT])

@@ -19,18 +19,15 @@ HID = 1024
 Y_DIM = 128
 CH = 512
 N_CH = N_S // CH
-N_UNITS = 4 * N_CH
 JT = N_S // P
 Y_PITCH = 144
+LV, MU = 0, 1
+RING = 3
+LAG = 0
+XQ_LATE = False
+V_FILLS = ((1, 0), (1, 1), (2, 0), (2, 1))
 
 FLOPS = 2 * N_S * (2 * X_DIM * HID + 2 * HID * Y_DIM)
-
-MANUAL = True
-LAG_C = 2
-LAG_D = 3
-LAG_E = 4
-V_STEPS = 3
-GRAM_0 = 2
 
 
 def tile_infoncemi_pa_t_kernel(
@@ -47,13 +44,12 @@ def tile_infoncemi_pa_t_kernel(
         keep = ctx.enter_context(tc.tile_pool(name="keep", bufs=1))
         work = ctx.enter_context(tc.tile_pool(name="work", bufs=2))
         psum = ctx.enter_context(tc.psum_pool(name="psum", bufs=1))
-        if MANUAL:
-            ctx.enter_context(tc.manual_schedule())
+        ctx.enter_context(tc.manual_schedule())
 
         x_sb = keep.tile([P, JT * X_DIM], BF16)
         xc = keep.tile([P, N_S], U32, align_bytes=64)
         xs = keep.tile([P, N_S], U8, align_bytes=64)
-        w1raw = [keep.tile([P, 4, HID], BF16, name="w1raw%d" % h) for h in range(2)]
+        w1raw = [[keep.tile([P, 4, 512], BF16, name="w1raw%d%d" % (h, g)) for g in range(2)] for h in range(2)]
         w1c = [keep.tile([P, HID], U32, name="w1c%d" % h, align_bytes=64) for h in range(2)]
         w1s = [keep.tile([P, HID], U8, name="w1s%d" % h, align_bytes=64) for h in range(2)]
         w2raw = [keep.tile([P, 8, Y_DIM], BF16, name="w2raw%d" % h) for h in range(2)]
@@ -65,22 +61,24 @@ def tile_infoncemi_pa_t_kernel(
         bias_sb = keep.tile([P, 32], F32)
         ident_f = keep.tile([P, P], F32)
         ident_b = keep.tile([P, P], BF16)
-        cred = keep.tile([P, 2], F32)
+        sel = [keep.tile([P, 2 * P], F32, name="sel%d" % o) for o in range(2)]
         stat = keep.tile([P, 8], F32)
-        r_sb = keep.tile([P, 2 * JT], F32)
+        r_sb = keep.tile([2 * N_CH, CH], F32)
         warm = keep.tile([P, 1], F32)
 
-        x_rows = x_samples.rearrange("(p j) k -> p (j k)", j=JT)
-
         def load_x(first_tile, n_tiles):
-            cols = slice(X_DIM * first_tile, X_DIM * (first_tile + n_tiles))
-            nc.sync.dma_start(out=x_sb[:, cols], in_=x_rows[:, cols])
+            c, j = divmod(first_tile, 4)
+            rows = x_samples[CH * c : CH * (c + 1), :].rearrange("(p j) k -> p (j k)", j=4)
+            nc.sync.dma_start(
+                out=x_sb[:, X_DIM * first_tile : X_DIM * (first_tile + n_tiles)],
+                in_=rows[:, X_DIM * j : X_DIM * (j + n_tiles)],
+            )
 
         def load_w1(h, g):
             cols = slice(512 * g, 512 * (g + 1))
             for u in range(2):
                 nc.sync.dma_start(
-                    out=w1raw[h][:, 2 * u : 2 * u + 2, cols],
+                    out=w1raw[h][g][:, 2 * u : 2 * u + 2, :],
                     in_=w1_dram[h][256 * u : 256 * (u + 1), cols].rearrange("(q e) c -> q e c", e=2),
                 )
 
@@ -91,28 +89,39 @@ def tile_infoncemi_pa_t_kernel(
             nc.scalar.dma_start(out=braw[8 * h : 8 * h + 8, :], in_=b1_dram[h].rearrange("(m p) -> m p", p=P))
         for h in range(2):
             nc.scalar.dma_start(out=braw[16 + h : 17 + h, :], in_=b2_dram[h].rearrange("(o p) -> o p", o=1))
-        load_w1(0, 0)
-        load_w1(0, 1)
+        load_w1(LV, 0)
+        load_w1(LV, 1)
         load_x(4, 4)
-        load_w1(1, 0)
-        load_w1(1, 1)
+        load_w1(MU, 0)
+        load_w1(MU, 1)
         nc.vector.memset(y_sb[:, :, Y_DIM:Y_PITCH], 1.0)
-        nc.sync.dma_start(out=y_sb[:, :, 0:Y_DIM], in_=y_samples.rearrange("(p j) d -> p j d", j=JT))
         for h in range(2):
             nc.sync.dma_start(out=w2raw[h][:], in_=w2_dram[h].rearrange("(m p) n -> p m n", p=P))
+        for c in range(N_CH):
+            nc.sync.dma_start(
+                out=y_sb[:, 4 * c : 4 * c + 4, 0:Y_DIM],
+                in_=y_samples[CH * c : CH * (c + 1), :].rearrange("(p j) d -> p j d", j=4),
+            )
         for c in range(2, N_CH):
             load_x(4 * c, 4)
 
         make_identity(nc, ident_f[:])
         make_identity(nc, ident_b[:])
-        nc.vector.memset(cred[:, 0:1], -0.5)
-        nc.vector.memset(cred[:, 1:2], -0.5 * inv_n)
-        nc.scalar.activation(out=warm[:], in_=cred[:, 0:1], func=ACT.Exp)
+        for o in range(2):
+            nc.gpsimd.memset(sel[o][:], 0.0)
+            nc.gpsimd.memset(sel[o][:, P : P + 1], -0.5 * (1.0, inv_n)[o])
+        nc.scalar.activation(out=warm[:], in_=ident_f[:, 0:1], func=ACT.Exp)
 
         x_words = x_sb[:].bitcast(F32)
 
-        def x_transposes(c, half, tag):
-            xt = psum.tile([P, 512], F32, tag=tag, name="xt")
+        n_side = [0]
+
+        def side_bank(shape, dtype, name):
+            n_side[0] += 1
+            return psum.tile(shape, dtype, tag="v%d" % (n_side[0] % 2), name=name)
+
+        def x_transposes(c, half):
+            xt = side_bank([P, 512], F32, "xt")
             for jj in range(2):
                 j = 4 * c + 2 * half + jj
                 for u in range(2):
@@ -131,11 +140,17 @@ def tile_infoncemi_pa_t_kernel(
             cols = slice(CH * c, CH * (c + 1))
             nc.vector.quantize_mx(out=xc[:, cols].bitcast(FP8X4), scales=xs[:, cols], in_=xg[:].bitcast(BF16))
 
+        def y_transposes(c):
+            yt = side_bank([P, 8 * P], BF16, "yt")
+            for i in range(8):
+                nc.tensor.transpose(yt[:, P * i : P * (i + 1)], y_sb[:, 4 * c + i, 0:Y_DIM], ident_b[:])
+            return yt
+
         def w1_regroup(h, g):
             wg = work.tile([P, 512, 4], BF16, tag="wg", name="wg", align_bytes=64)
             nc.vector.tensor_copy(
                 out=wg[:].rearrange("p (c i) t -> p c t i", i=4),
-                in_=w1raw[h][:, :, 512 * g : 512 * (g + 1)].rearrange("p t (c i) -> p c t i", i=4),
+                in_=w1raw[h][g][:].rearrange("p t (c i) -> p c t i", i=4),
             )
             return wg
 
@@ -155,38 +170,32 @@ def tile_infoncemi_pa_t_kernel(
                 out=w2c[h][:].bitcast(FP8X4), scales=w2s[h][:], in_=w2g[:].rearrange("p g n t -> p (g n t)")
             )
 
-        xg_tiles = {}
-        xg_tiles[0] = work.tile([P, 2 * CH], F32, tag="xg", name="xg", align_bytes=64)
-        for half in range(2):
-            x_evac(xg_tiles[0], half, x_transposes(0, half, "s1_%d" % half))
-        bt_ps = psum.tile([P, P], BF16, tag="mx", name="bt_ps")
-        nc.tensor.transpose(bt_ps[:], braw[:], ident_b[:])
-        wg0 = w1_regroup(0, 0)
-        nc.vector.tensor_copy(out=bias_sb[:], in_=bt_ps[:, 0:32])
-        w1_quant(0, 0, wg0)
-        x_quant(0, xg_tiles[0])
+        steps = [(0, h, g) for h in range(2) for g in range(2)]
+        for c in range(1, N_CH):
+            steps += [(c, LV, 0), (c, MU, 0), (c, MU, 1)]
+        n_steps = len(steps)
+
+        def has_v(c):
+            return 1 <= c < N_CH
+
+        first = [steps.index((c, LV, 0)) for c in range(N_CH)] + [n_steps]
 
         banks = {}
         hc = {}
         hg = {}
         hq = {}
         hs = {}
+        hp = {}
+        pb = {}
         acc = {}
         ep = {}
-        misc = {}
+        left = {}
+        misc = {"ring": 0, "sums": 0}
 
-        def unit(n):
-            c, k = divmod(n, 4)
-            return c, k // 2, k % 2
-
-        def stage1(n, t):
-            c, h, g = unit(n)
-            bank = psum.tile([P, CH], F32, tag="s1_%d" % t, name="bank")
-            banks[(n, t)] = bank
-            wcols = slice(512 * g + 128 * t, 512 * g + 128 * (t + 1))
-            xcols = slice(CH * c, CH * (c + 1))
+        def mx1(out, h, col, xcols):
+            wcols = slice(col, col + P)
             nc.tensor.matmul_mx(
-                out=bank[:],
+                out=out,
                 lhsT=w1c[h][:, wcols].bitcast(FP8X4),
                 lhsT_scale=w1s[h][:, wcols],
                 rhs=xc[:, xcols].bitcast(FP8X4),
@@ -195,47 +204,70 @@ def tile_infoncemi_pa_t_kernel(
                 stop=True,
             )
 
-        def evac(n, t, on_vector):
-            c, h, g = unit(n)
+        def fill(k, t):
+            c, h, g = steps[k]
+            misc["ring"] += 1
+            banks[(k, t)] = psum.tile([P, CH], F32, tag="s%d" % (misc["ring"] % RING), name="bank")
+            mx1(banks[(k, t)][:], h, 512 * g + P * t, slice(CH * c, CH * (c + 1)))
+
+        def evac(k, t):
+            c, h, g = steps[k]
             if t == 0:
-                hc[n] = work.tile([P, 4, CH], BF16, tag="hc", name="hc", bufs=LAG_C + 2)
+                hc[k] = work.tile([P, 4, CH], BF16, tag="hc", name="hc", bufs=3)
             col = 8 * h + 4 * g + t
-            bank = banks[(n, t)]
-            if on_vector:
-                nc.vector.tensor_scalar(
-                    out=hc[n][:, t, :], in0=bank[:], scalar1=bias_sb[:, col : col + 1], scalar2=0.0,
-                    op0=ALU.add, op1=ALU.max,
-                )
-            else:
-                nc.scalar.activation(out=hc[n][:, t, :], in_=bank[:], func=ACT.Relu, bias=bias_sb[:, col : col + 1])
+            nc.scalar.activation(
+                out=hc[k][:, t, :], in_=banks[(k, t)][:], func=ACT.Relu, bias=bias_sb[:, col : col + 1]
+            )
 
-        def regroup(n):
-            hg[n] = work.tile([P, CH, 4], BF16, tag="hg", name="hg", align_bytes=64)
+        def regroup(k):
+            hg[k] = work.tile([P, CH, 4], BF16, tag="hg", name="hg", align_bytes=64)
             nc.vector.tensor_copy(
-                out=hg[n][:].rearrange("p (c i) t -> p c t i", i=4),
-                in_=hc[n][:].rearrange("p t (c i) -> p c t i", i=4),
+                out=hg[k][:].rearrange("p (c i) t -> p c t i", i=4),
+                in_=hc[k][:].rearrange("p t (c i) -> p c t i", i=4),
             )
 
-        def quant(n):
-            hq[n] = work.tile([P, CH], U32, tag="hq", name="hq", align_bytes=64, bufs=3)
-            hs[n] = work.tile([P, CH], U8, tag="hs", name="hs", align_bytes=64, bufs=3)
+        def quant(key, grouped):
+            hq[key] = work.tile([P, CH], U32, tag="hq", name="hq", align_bytes=64, bufs=4)
+            hs[key] = work.tile([P, CH], U8, tag="hs", name="hs", align_bytes=64, bufs=4)
             nc.vector.quantize_mx(
-                out=hq[n][:].bitcast(FP8X4), scales=hs[n][:], in_=hg[n][:].rearrange("p c t -> p (c t)")
+                out=hq[key][:].bitcast(FP8X4), scales=hs[key][:], in_=grouped[:].rearrange("p c t -> p (c t)")
             )
 
-        def stage2(n):
-            c, h, g = unit(n)
-            if g == 0:
+        def fill_v(c, b):
+            pb[(c, b)] = side_bank([P, CH], F32, "pb")
+            lo = CH * c + P * b
+            for t in range(4):
+                mx1(pb[(c, b)][:, P * t : P * (t + 1)], LV, 512 + P * t, slice(lo, lo + P))
+
+        def evac_v(c, b):
+            if b == 0:
+                hp[c] = work.tile([P, CH, 4], BF16, tag="hp", name="hp", align_bytes=64)
+            nc.vector.tensor_tensor(
+                out=hp[c][:, P * b : P * (b + 1), :],
+                in0=pb[(c, b)][:].rearrange("p (t n) -> p n t", t=4),
+                in1=bias_sb[:, 4:8].unsqueeze(1).to_broadcast([P, P, 4]),
+                op=ALU.add,
+            )
+
+        def relu_v(c):
+            flat = hp[c][:].rearrange("p c t -> p (c t)")
+            nc.vector.tensor_scalar(out=flat, in0=flat, scalar1=0.0, scalar2=None, op0=ALU.max)
+
+        def stage2(key, c, h, g):
+            opens = (c, h) not in left
+            if opens:
+                left[(c, h)] = 2
                 acc[(c, h)] = psum.tile([P, CH], F32, tag="acc%d" % h, name="acc")
+            left[(c, h)] -= 1
             cols = slice(Y_DIM * g, Y_DIM * (g + 1))
             nc.tensor.matmul_mx(
                 out=acc[(c, h)][:],
                 lhsT=w2c[h][:, cols].bitcast(FP8X4),
                 lhsT_scale=w2s[h][:, cols],
-                rhs=hq[n][:].bitcast(FP8X4),
-                rhs_scale=hs[n][:],
-                start=(g == 0),
-                stop=(g == 1),
+                rhs=hq[key][:].bitcast(FP8X4),
+                rhs_scale=hs[key][:],
+                start=opens,
+                stop=left[(c, h)] == 0,
             )
 
         def ep_tile(c, what):
@@ -243,22 +275,22 @@ def tile_infoncemi_pa_t_kernel(
             return ep[(c, what)]
 
         def tanh_lv(c):
-            nc.scalar.activation(out=ep_tile(c, "th")[:], in_=acc[(c, 0)][:], func=ACT.Tanh, bias=bias_sb[:, 16:17])
+            nc.scalar.activation(out=ep_tile(c, "th")[:], in_=acc[(c, LV)][:], func=ACT.Tanh, bias=bias_sb[:, 16:17])
 
         def exp_w(c):
             nc.scalar.activation(out=ep_tile(c, "w")[:], in_=ep[(c, "th")][:], func=ACT.Exp, scale=-1.0)
 
         def sq_e(c):
-            nc.scalar.activation(out=ep_tile(c, "e2")[:], in_=acc[(c, 1)][:], func=ACT.Square, bias=stat[:, 2:3])
+            nc.scalar.activation(out=ep_tile(c, "e2")[:], in_=acc[(c, MU)][:], func=ACT.Square, bias=stat[:, 2:3])
 
         def diff_d(c):
             nc.vector.scalar_tensor_tensor(
-                out=ep_tile(c, "d")[:], in0=acc[(c, 1)][:], scalar=bias_sb[:, 17:18],
+                out=ep_tile(c, "d")[:], in0=acc[(c, MU)][:], scalar=bias_sb[:, 17:18],
                 in1=yT[:, CH * c : CH * (c + 1)], op0=ALU.add, op1=ALU.subtract,
             )
 
         def sq_d(c):
-            nc.scalar.activation(out=ep_tile(c, "d2")[:], in_=ep[(c, "d")][:], func=ACT.Square)
+            nc.gpsimd.tensor_tensor(out=ep_tile(c, "d2")[:], in0=ep[(c, "d")][:], in1=ep[(c, "d")][:], op=ALU.mult)
 
         def sq_d_on_vector(c):
             nc.vector.tensor_tensor(out=ep_tile(c, "d2")[:], in0=ep[(c, "d")][:], in1=ep[(c, "d")][:], op=ALU.mult)
@@ -270,124 +302,167 @@ def tile_infoncemi_pa_t_kernel(
             )
 
         def term_p(c):
+            nc.gpsimd.tensor_tensor(out=ep_tile(c, "p")[:], in0=ep[(c, "d2")][:], in1=ep[(c, "w")][:], op=ALU.mult)
+
+        def term_p_on_vector(c):
             nc.vector.tensor_tensor(out=ep_tile(c, "p")[:], in0=ep[(c, "d2")][:], in1=ep[(c, "w")][:], op=ALU.mult)
 
         def sums_over_d(c, what):
             o = 0 if what == "p" else 1
-            term = ep[(c, what)]
-            for j in range(4):
-                col = JT * o + 4 * c + j
+            row = N_CH * o + c
+            if misc["sums"] == 0:
+                misc["r"] = psum.tile([P, CH], F32, tag="mr", name="r_ps")
+            misc["sums"] += 1
+            nc.tensor.matmul(
+                out=misc["r"][:], lhsT=sel[o][:, P - row : 2 * P - row], rhs=ep[(c, what)][:],
+                start=(misc["sums"] == 1), stop=(misc["sums"] == 2 * N_CH),
+            )
+
+        def gram(part):
+            if part == 0:
+                misc["g"] = psum.tile([P, CH], F32, tag="mr", name="g_ps")
+            for i in range(8):
+                j = 8 * part + i
                 nc.tensor.matmul(
-                    out=misc["r"][:, col : col + 1], lhsT=term[:, P * j : P * (j + 1)], rhs=cred[:, o : o + 1],
-                    start=True, stop=True,
+                    out=misc["g"][:, 0 : Y_DIM + 2], lhsT=y_sb[:, j, 0:Y_DIM], rhs=y_sb[:, j, 0 : Y_DIM + 2],
+                    start=(j == 0), stop=(j == JT - 1),
                 )
 
-        def sums_q(c):
-            sums_over_d(c, "q")
+        def statistics():
+            g_ps = misc["g"]
+            gd = work.tile([P, P], F32, tag="gd", name="gd")
+            nc.vector.tensor_tensor(out=gd[:], in0=g_ps[:, 0:P], in1=ident_f[:], op=ALU.mult)
+            nc.vector.tensor_scalar(
+                out=stat[:, 1:2], in0=g_ps[:, P : P + 1], scalar1=inv_n, scalar2=None, op0=ALU.mult
+            )
+            nc.vector.reduce_sum(out=stat[:, 0:1], in_=gd[:], axis=AX.X)
+            nc.vector.tensor_tensor(out=stat[:, 2:3], in0=bias_sb[:, 17:18], in1=stat[:, 1:2], op=ALU.subtract)
+            nc.vector.tensor_tensor(out=stat[:, 3:4], in0=stat[:, 1:2], in1=stat[:, 1:2], op=ALU.mult)
+            nc.vector.scalar_tensor_tensor(
+                out=stat[:, 4:5], in0=stat[:, 0:1], scalar=inv_n, in1=stat[:, 3:4], op0=ALU.mult, op1=ALU.subtract
+            )
 
-        def sums_p(c):
-            sums_over_d(c, "p")
+        xt = {}
+        xg = {}
 
-        def run_due(s, table):
-            for offset, op in table:
-                k, rem = divmod(s - offset, 4)
-                if rem == 0 and 0 <= k < N_CH - 1:
-                    op(k)
+        def x_first_evac(c, half):
+            if half == 0:
+                xg[c] = work.tile([P, 2 * CH], F32, tag="xg", name="xg", align_bytes=64)
+            x_evac(xg[c], half, xt.pop((c, half)))
+
+        for half in range(2):
+            xt[(0, half)] = x_transposes(0, half)
+            x_first_evac(0, half)
+        x_quant(0, xg[0])
+        bt_ps = side_bank([P, P], BF16, "bt_ps")
+        nc.tensor.transpose(bt_ps[:], braw[:], ident_b[:])
+        wg = w1_regroup(LV, 0)
+        nc.vector.tensor_copy(out=bias_sb[:], in_=bt_ps[:, 0:32])
+        w1_quant(LV, 0, wg)
+        wg = w1_regroup(LV, 1)
+        w1_quant(LV, 1, wg)
+
+        def phase(k):
+            if k >= n_steps:
+                return N_CH, k - n_steps
+            if k < 0:
+                return -1, 0
+            return steps[k][0], k - first[steps[k][0]]
 
         last = N_CH - 1
-        for s in range(N_UNITS + LAG_E):
-            c, r = divmod(s, 4)
-            live = s < N_UNITS
-            cn = c + 1
+        for n in range(RING):
+            fill(*divmod(n, 4))
+        for k in range(n_steps + 2 + LAG):
+            c, i = phase(k)
+            kv = k - LAG
+            cv, iv = phase(kv)
+            prev = cv - 1
+            nxt = c + 1 if 0 <= c < last else None
+            x_step = 1 if c == 0 else 0
 
-            if live:
-                stage1(s, 0)
-            if s >= LAG_E:
-                stage2(s - LAG_E)
-            if live:
-                for t in range(1, 4):
-                    stage1(s, t)
-            if s == LAG_E + 6:
-                misc["r"] = psum.tile([P, 2 * JT], F32, tag="mr", name="r_ps")
-            run_due(s, ((LAG_E + 6, sums_q), (LAG_E + 7, sums_p)))
-            x_fill = live and cn < N_CH and r < 2
-            y_fill = live and r == 2 and c % 2 == 0
-            if x_fill:
-                fill = x_transposes(cn, r, "mx")
-            if y_fill:
-                fill = psum.tile([P, 8 * P], BF16, tag="mx", name="yt")
-                for i in range(8):
-                    nc.tensor.transpose(fill[:, P * i : P * (i + 1)], y_sb[:, 4 * c + i, 0:Y_DIM], ident_b[:])
-            if GRAM_0 <= s < GRAM_0 + 4:
-                if s == GRAM_0:
-                    g_ps = psum.tile([P, 256], F32, tag="mr", name="g_ps")
-                for i in range(8):
-                    j = 8 * (s - GRAM_0) + i
-                    nc.tensor.matmul(
-                        out=g_ps[:, 0 : Y_DIM + 2], lhsT=y_sb[:, j, 0:Y_DIM], rhs=y_sb[:, j, 0 : Y_DIM + 2],
-                        start=(j == 0), stop=(j == JT - 1),
-                    )
+            for t in range(4):
+                if t == 0 and iv == 2 and 1 <= cv < N_CH:
+                    exp_w(prev)
+                if k < n_steps:
+                    evac(k, t)
+                if nxt and i == x_step and t >= 2:
+                    x_first_evac(nxt, t - 2)
+                if t == 2 and iv == 1 and cv >= 1:
+                    tanh_lv(prev)
+                if i == 1 and t == 1 and c % 2 == 1:
+                    nc.scalar.copy(out=yT[:, CH * (c - 1) : CH * (c + 1)], in_=misc["yt"][:])
 
-            if live:
-                run_due(s, ((LAG_E + 4, diff_d),))
-            wnext = {0: (0, 1), 1: (1, 0), 2: (1, 1)}.get(s)
-            if wnext is not None:
-                wg = w1_regroup(wnext[0], wnext[1])
-            if s in (2, 3):
-                w2g = w2_regroup(s - 2)
-            if 0 <= s - LAG_D < N_UNITS:
-                quant(s - LAG_D)
-            if wnext is not None:
-                w1_quant(wnext[0], wnext[1], wg)
-            if s in (2, 3):
-                w2_quant(s - 2, w2g)
-            if 0 <= s - LAG_C < N_UNITS:
-                regroup(s - LAG_C)
-            if not live:
-                run_due(s, ((LAG_E + 4, diff_d),))
-            if s == GRAM_0 + 5:
-                gd = work.tile([P, P], F32, tag="gd", name="gd")
-                nc.vector.tensor_tensor(out=gd[:], in0=g_ps[:, 0:P], in1=ident_f[:], op=ALU.mult)
-                nc.vector.reduce_sum(out=stat[:, 0:1], in_=gd[:], axis=AX.X)
-                nc.vector.tensor_scalar(
-                    out=stat[:, 1:2], in0=g_ps[:, P : P + 1], scalar1=inv_n, scalar2=None, op0=ALU.mult
-                )
-                nc.vector.tensor_tensor(out=stat[:, 2:3], in0=bias_sb[:, 17:18], in1=stat[:, 1:2], op=ALU.subtract)
-                nc.vector.tensor_tensor(out=stat[:, 3:4], in0=stat[:, 1:2], in1=stat[:, 1:2], op=ALU.mult)
-                nc.vector.scalar_tensor_tensor(
-                    out=stat[:, 4:5], in0=stat[:, 0:1], scalar=inv_n, in1=stat[:, 3:4], op0=ALU.mult, op1=ALU.subtract
-                )
+                ahead = 4 * k + t + RING
+                if ahead < 4 * n_steps:
+                    fill(*divmod(ahead, 4))
+                if nxt and i == x_step and t < 2:
+                    xt[(nxt, t)] = x_transposes(nxt, t)
+                if i == 0 and t == 3 and c % 2 == 1:
+                    misc["yt"] = y_transposes(c - 1)
+                if iv == 1 and t == 0 and has_v(prev):
+                    stage2(("v", prev), prev, LV, 1)
+                if t == 2 and 0 <= kv - 2 < n_steps:
+                    stage2(kv - 2, *steps[kv - 2])
+                if has_v(cv) and (iv, t) in V_FILLS:
+                    fill_v(cv, V_FILLS.index((iv, t)))
+                if cv >= 2 and iv == 0 and t == 3:
+                    sums_over_d(cv - 2, "p")
+                if cv >= 2 and iv == 1 and t == 1:
+                    sums_over_d(cv - 2, "q")
+                if k == 4:
+                    gram(t)
 
-            v_bank = live and c >= 1 and r < V_STEPS
-            if live:
-                for t in range(3 if v_bank else 4):
-                    evac(s, t, False)
-            run_due(s, ((LAG_E + 2, tanh_lv), (LAG_E + 3, exp_w), (LAG_E + 4, sq_e), (LAG_E + 5, sq_d)))
-            if s == 4 * last + LAG_E + 2:
-                tanh_lv(last)
-            if s == 4 * last + LAG_E + 3:
-                exp_w(last)
-            if x_fill:
-                if r == 0:
-                    xg_tiles[cn] = work.tile([P, 2 * CH], F32, tag="xg", name="xg", align_bytes=64)
-                x_evac(xg_tiles[cn], r, fill)
-            if y_fill:
-                nc.scalar.copy(out=yT[:, CH * c : CH * (c + 2)], in_=fill[:])
+            if nxt and i == x_step + 1 and not XQ_LATE:
+                x_quant(nxt, xg[nxt])
+            if 0 <= kv - 1 < n_steps:
+                regroup(kv - 1)
+            if k == 0:
+                wg = w1_regroup(MU, 0)
+                w1_quant(MU, 0, wg)
+            if k == 1:
+                wg = w1_regroup(MU, 1)
+                w2g = w2_regroup(LV)
+                w1_quant(MU, 1, wg)
+                w2_quant(LV, w2g)
+            if k == 2:
+                w2g = w2_regroup(MU)
+            if k == 5:
+                statistics()
+            if iv == 0 and cv >= 2:
+                term_q(cv - 2)
+            if iv == 0 and has_v(prev):
+                quant(("v", prev), hp[prev])
+            if iv == 2 and 1 <= cv < N_CH:
+                diff_d(prev)
+                sq_d(prev)
+                term_p(prev)
+            if iv in (1, 2) and has_v(cv):
+                for b in (2 * iv - 2, 2 * iv - 1):
+                    evac_v(cv, b)
+            if iv == 2 and has_v(cv):
+                relu_v(cv)
+            if 0 <= kv - 1 < n_steps:
+                quant(kv - 1, hg[kv - 1])
+            if k == 2:
+                w2_quant(MU, w2g)
+            if nxt and i == x_step + 1 and XQ_LATE:
+                x_quant(nxt, xg[nxt])
 
-            run_due(s, ((LAG_E + 5, term_q), (LAG_E + 6, term_p)))
-            if live and cn < N_CH and r == 2:
-                x_quant(cn, xg_tiles[cn])
-            if v_bank:
-                evac(s, 3, True)
+            if iv == 2 and 1 <= cv < N_CH:
+                sq_e(prev)
 
+        exp_w(last)
         diff_d(last)
         sq_e(last)
         sq_d_on_vector(last)
-        term_p(last)
-        sums_p(last)
+        term_p_on_vector(last)
+        sums_over_d(last, "p")
         term_q(last)
-        sums_q(last)
+        sums_over_d(last, "q")
 
-        nc.vector.tensor_copy(out=r_sb[:], in_=misc["r"][:])
-        nc.sync.dma_start(out=out_0.rearrange("(p j) -> p j", j=JT), in_=r_sb[:, 0:JT])
-        nc.sync.dma_start(out=out_1.rearrange("(p j) -> p j", j=JT), in_=r_sb[:, JT : 2 * JT])
+        nc.vector.tensor_copy(
+            out=r_sb[:].rearrange("c (s j) -> c s j", j=4),
+            in_=misc["r"][0 : 2 * N_CH, :].rearrange("c (j s) -> c s j", j=4),
+        )
+        nc.sync.dma_start(out=out_0.rearrange("(c i) -> c i", i=CH), in_=r_sb[0:N_CH, :])
+        nc.sync.dma_start(out=out_1.rearrange("(c i) -> c i", i=CH), in_=r_sb[N_CH : 2 * N_CH, :])

@@ -290,7 +290,7 @@ def tile_infoncemi_pa_t_kernel(
             )
 
         def sq_d(c):
-            nc.gpsimd.tensor_tensor(out=ep_tile(c, "d2")[:], in0=ep[(c, "d")][:], in1=ep[(c, "d")][:], op=ALU.mult)
+            nc.scalar.activation(out=ep_tile(c, "d2")[:], in_=ep[(c, "d")][:], func=ACT.Square)
 
         def sq_d_on_vector(c):
             nc.vector.tensor_tensor(out=ep_tile(c, "d2")[:], in0=ep[(c, "d")][:], in1=ep[(c, "d")][:], op=ALU.mult)
@@ -302,7 +302,7 @@ def tile_infoncemi_pa_t_kernel(
             )
 
         def term_p(c):
-            nc.gpsimd.tensor_tensor(out=ep_tile(c, "p")[:], in0=ep[(c, "d2")][:], in1=ep[(c, "w")][:], op=ALU.mult)
+            nc.vector.tensor_tensor(out=ep_tile(c, "p")[:], in0=ep[(c, "d2")][:], in1=ep[(c, "w")][:], op=ALU.mult)
 
         def term_p_on_vector(c):
             nc.vector.tensor_tensor(out=ep_tile(c, "p")[:], in0=ep[(c, "d2")][:], in1=ep[(c, "w")][:], op=ALU.mult)

@@ -17,15 +17,15 @@ N_S = 4096
 X_DIM = 512
 HID = 1024
 Y_DIM = 128
-CH = 512
-N_CH = N_S // CH
+BANK = 512
 JT = N_S // P
+N_ROWS = N_S // BANK
 Y_PITCH = 144
 LV, MU = 0, 1
-RING = 3
-LAG = 0
-XQ_LATE = False
-V_FILLS = ((1, 0), (1, 1), (2, 0), (2, 1))
+CHUNKS = [(BANK * c, BANK) for c in range(7)] + [(7 * BANK, 256), (7 * BANK + 256, 256)]
+NC = len(CHUNKS)
+V_CHUNKS = range(1, 7)
+RING = 4
 
 FLOPS = 2 * N_S * (2 * X_DIM * HID + 2 * HID * Y_DIM)
 
@@ -58,17 +58,19 @@ def tile_infoncemi_pa_t_kernel(
         y_sb = keep.tile([P, JT, Y_PITCH], BF16)
         yT = keep.tile([P, N_S], BF16)
         braw = keep.tile([P, P], BF16)
-        bias_sb = keep.tile([P, 32], F32)
+        braw2 = keep.tile([P, P], BF16)
+        bias_sb = keep.tile([P, 16], F32)
+        bias2_sb = keep.tile([P, 2], F32)
         ident_f = keep.tile([P, P], F32)
         ident_b = keep.tile([P, P], BF16)
         sel = [keep.tile([P, 2 * P], F32, name="sel%d" % o) for o in range(2)]
         stat = keep.tile([P, 8], F32)
-        r_sb = keep.tile([2 * N_CH, CH], F32)
+        r_sb = keep.tile([2 * N_ROWS, BANK], F32)
         warm = keep.tile([P, 1], F32)
 
         def load_x(first_tile, n_tiles):
             c, j = divmod(first_tile, 4)
-            rows = x_samples[CH * c : CH * (c + 1), :].rearrange("(p j) k -> p (j k)", j=4)
+            rows = x_samples[BANK * c : BANK * (c + 1), :].rearrange("(p j) k -> p (j k)", j=4)
             nc.sync.dma_start(
                 out=x_sb[:, X_DIM * first_tile : X_DIM * (first_tile + n_tiles)],
                 in_=rows[:, X_DIM * j : X_DIM * (j + n_tiles)],
@@ -82,27 +84,28 @@ def tile_infoncemi_pa_t_kernel(
                     in_=w1_dram[h][256 * u : 256 * (u + 1), cols].rearrange("(q e) c -> q e c", e=2),
                 )
 
+        nc.vector.memset(braw[:], 0.0)
         load_x(0, 2)
         load_x(2, 2)
-        nc.vector.memset(braw[:], 0.0)
-        for h in range(2):
-            nc.scalar.dma_start(out=braw[8 * h : 8 * h + 8, :], in_=b1_dram[h].rearrange("(m p) -> m p", p=P))
-        for h in range(2):
-            nc.scalar.dma_start(out=braw[16 + h : 17 + h, :], in_=b2_dram[h].rearrange("(o p) -> o p", o=1))
         load_w1(LV, 0)
         load_w1(LV, 1)
-        load_x(4, 4)
+        for h in range(2):
+            nc.scalar.dma_start(out=braw[8 * h : 8 * h + 8, :], in_=b1_dram[h].rearrange("(m p) -> m p", p=P))
         load_w1(MU, 0)
+        load_x(4, 4)
         load_w1(MU, 1)
         nc.vector.memset(y_sb[:, :, Y_DIM:Y_PITCH], 1.0)
+        nc.vector.memset(braw2[:], 0.0)
         for h in range(2):
             nc.sync.dma_start(out=w2raw[h][:], in_=w2_dram[h].rearrange("(m p) n -> p m n", p=P))
-        for c in range(N_CH):
+        for h in range(2):
+            nc.sync.dma_start(out=braw2[h : h + 1, :], in_=b2_dram[h].rearrange("(o p) -> o p", o=1))
+        for c in range(N_ROWS):
             nc.sync.dma_start(
                 out=y_sb[:, 4 * c : 4 * c + 4, 0:Y_DIM],
-                in_=y_samples[CH * c : CH * (c + 1), :].rearrange("(p j) d -> p j d", j=4),
+                in_=y_samples[BANK * c : BANK * (c + 1), :].rearrange("(p j) d -> p j d", j=4),
             )
-        for c in range(2, N_CH):
+        for c in range(2, N_ROWS):
             load_x(4 * c, 4)
 
         make_identity(nc, ident_f[:])
@@ -114,44 +117,14 @@ def tile_infoncemi_pa_t_kernel(
 
         x_words = x_sb[:].bitcast(F32)
 
-        n_side = [0]
-
-        def side_bank(shape, dtype, name):
-            n_side[0] += 1
-            return psum.tile(shape, dtype, tag="v%d" % (n_side[0] % 2), name=name)
-
-        def x_transposes(c, half):
-            xt = side_bank([P, 512], F32, "xt")
-            for jj in range(2):
-                j = 4 * c + 2 * half + jj
-                for u in range(2):
-                    nc.tensor.transpose(
-                        xt[:, 128 * (2 * jj + u) : 128 * (2 * jj + u + 1)],
-                        x_words[:, 256 * j + 128 * u : 256 * j + 128 * (u + 1)],
-                        ident_f[:],
-                    )
-            return xt
-
-        def x_evac(xg, half, xt):
-            dst = xg[:].rearrange("q (j s u) -> q j s u", j=4, s=P, u=2)[:, 2 * half : 2 * half + 2]
-            nc.scalar.copy(out=dst, in_=xt[:].rearrange("q (j u s) -> q j s u", j=2, u=2, s=P))
-
-        def x_quant(c, xg):
-            cols = slice(CH * c, CH * (c + 1))
-            nc.vector.quantize_mx(out=xc[:, cols].bitcast(FP8X4), scales=xs[:, cols], in_=xg[:].bitcast(BF16))
-
-        def y_transposes(c):
-            yt = side_bank([P, 8 * P], BF16, "yt")
-            for i in range(8):
-                nc.tensor.transpose(yt[:, P * i : P * (i + 1)], y_sb[:, 4 * c + i, 0:Y_DIM], ident_b[:])
-            return yt
-
-        def w1_regroup(h, g):
-            wg = work.tile([P, 512, 4], BF16, tag="wg", name="wg", align_bytes=64)
-            nc.vector.tensor_copy(
-                out=wg[:].rearrange("p (c i) t -> p c t i", i=4),
-                in_=w1raw[h][g][:].rearrange("p t (c i) -> p c t i", i=4),
-            )
+        def w1_regroup(h, g, engine):
+            wg = work.tile([P, 512, 4], BF16, tag="wg", name="wg", align_bytes=64, bufs=2)
+            dst = wg[:].rearrange("p (c i) t -> p c t i", i=4)
+            src = w1raw[h][g][:].rearrange("p t (c i) -> p c t i", i=4)
+            if engine == "s":
+                nc.scalar.copy(out=dst, in_=src)
+            else:
+                nc.vector.tensor_copy(out=dst, in_=src)
             return wg
 
         def w1_quant(h, g, wg):
@@ -170,17 +143,8 @@ def tile_infoncemi_pa_t_kernel(
                 out=w2c[h][:].bitcast(FP8X4), scales=w2s[h][:], in_=w2g[:].rearrange("p g n t -> p (g n t)")
             )
 
-        steps = [(0, h, g) for h in range(2) for g in range(2)]
-        for c in range(1, N_CH):
-            steps += [(c, LV, 0), (c, MU, 0), (c, MU, 1)]
-        n_steps = len(steps)
-
-        def has_v(c):
-            return 1 <= c < N_CH
-
-        first = [steps.index((c, LV, 0)) for c in range(N_CH)] + [n_steps]
-
         banks = {}
+        xg = {}
         hc = {}
         hg = {}
         hq = {}
@@ -191,6 +155,9 @@ def tile_infoncemi_pa_t_kernel(
         ep = {}
         left = {}
         misc = {"ring": 0, "sums": 0}
+
+        def cols_of(c):
+            return slice(CHUNKS[c][0], CHUNKS[c][0] + CHUNKS[c][1])
 
         def mx1(out, h, col, xcols):
             wcols = slice(col, col + P)
@@ -204,44 +171,75 @@ def tile_infoncemi_pa_t_kernel(
                 stop=True,
             )
 
-        def fill(k, t):
-            c, h, g = steps[k]
+        def fill(item):
+            kind, key, t = item
             misc["ring"] += 1
-            banks[(k, t)] = psum.tile([P, CH], F32, tag="s%d" % (misc["ring"] % RING), name="bank")
-            mx1(banks[(k, t)][:], h, 512 * g + P * t, slice(CH * c, CH * (c + 1)))
+            tag = "s%d" % (misc["ring"] % RING)
+            if kind == "u":
+                c, h, g = key
+                banks[item] = psum.tile([P, CHUNKS[c][1]], F32, tag=tag, name="bank")
+                mx1(banks[item][:], h, 512 * g + P * t, cols_of(c))
+            elif kind == "x":
+                banks[item] = psum.tile([P, BANK], F32, tag=tag, name="bank")
+                for n in range(4):
+                    lo = 2 * CHUNKS[key][0] + 512 * t + P * n
+                    nc.tensor.transpose(banks[item][:, P * n : P * (n + 1)], x_words[:, lo : lo + P], ident_f[:])
+            else:
+                banks[item] = psum.tile([P, 8 * P], BF16, tag=tag, name="bank")
+                for n in range(8):
+                    nc.tensor.transpose(banks[item][:, P * n : P * (n + 1)], y_sb[:, key + n, 0:Y_DIM], ident_b[:])
 
-        def evac(k, t):
-            c, h, g = steps[k]
-            if t == 0:
-                hc[k] = work.tile([P, 4, CH], BF16, tag="hc", name="hc", bufs=3)
-            col = 8 * h + 4 * g + t
-            nc.scalar.activation(
-                out=hc[k][:, t, :], in_=banks[(k, t)][:], func=ACT.Relu, bias=bias_sb[:, col : col + 1]
-            )
+        def empty(item):
+            kind, key, t = item
+            bank = banks.pop(item)
+            if kind == "u":
+                c, h, g = key
+                if t == 0:
+                    hc[key] = work.tile([P, 4, CHUNKS[c][1]], BF16, tag="hc", name="hc", bufs=4)
+                col = 8 * h + 4 * g + t
+                nc.scalar.activation(
+                    out=hc[key][:, t, :], in_=bank[:], func=ACT.Relu, bias=bias_sb[:, col : col + 1]
+                )
+            elif kind == "x":
+                if t == 0:
+                    xg[key] = work.tile([P, 2 * CHUNKS[key][1]], F32, tag="xg", name="xg", align_bytes=64)
+                nc.scalar.copy(
+                    out=xg[key][:, BANK * t : BANK * (t + 1)].rearrange("q (j s u) -> q j s u", j=2, u=2),
+                    in_=bank[:].rearrange("q (j u s) -> q j s u", j=2, u=2),
+                )
+            else:
+                nc.scalar.copy(out=yT[:, P * key : P * (key + 8)], in_=bank[:])
 
-        def regroup(k):
-            hg[k] = work.tile([P, CH, 4], BF16, tag="hg", name="hg", align_bytes=64)
-            nc.vector.tensor_copy(
-                out=hg[k][:].rearrange("p (c i) t -> p c t i", i=4),
-                in_=hc[k][:].rearrange("p t (c i) -> p c t i", i=4),
-            )
-
-        def quant(key, grouped):
-            hq[key] = work.tile([P, CH], U32, tag="hq", name="hq", align_bytes=64, bufs=4)
-            hs[key] = work.tile([P, CH], U8, tag="hs", name="hs", align_bytes=64, bufs=4)
+        def x_quant(c):
             nc.vector.quantize_mx(
-                out=hq[key][:].bitcast(FP8X4), scales=hs[key][:], in_=grouped[:].rearrange("p c t -> p (c t)")
+                out=xc[:, cols_of(c)].bitcast(FP8X4), scales=xs[:, cols_of(c)], in_=xg[c][:].bitcast(BF16)
+            )
+
+        def regroup(unit):
+            hg[unit] = work.tile([P, CHUNKS[unit[0]][1], 4], BF16, tag="hg", name="hg", align_bytes=64)
+            nc.vector.tensor_copy(
+                out=hg[unit][:].rearrange("p (c i) t -> p c t i", i=4),
+                in_=hc[unit][:].rearrange("p t (c i) -> p c t i", i=4),
+            )
+
+        def quant(unit):
+            c = unit[0]
+            grouped = hp[c] if c in V_CHUNKS and unit[1:] == (LV, 1) else hg[unit]
+            hq[unit] = work.tile([P, CHUNKS[c][1]], U32, tag="hq", name="hq", align_bytes=64, bufs=4)
+            hs[unit] = work.tile([P, CHUNKS[c][1]], U8, tag="hs", name="hs", align_bytes=64, bufs=4)
+            nc.vector.quantize_mx(
+                out=hq[unit][:].bitcast(FP8X4), scales=hs[unit][:], in_=grouped[:].rearrange("p c t -> p (c t)")
             )
 
         def fill_v(c, b):
-            pb[(c, b)] = side_bank([P, CH], F32, "pb")
-            lo = CH * c + P * b
+            pb[(c, b)] = psum.tile([P, BANK], F32, tag="v", name="pb")
+            lo = CHUNKS[c][0] + P * b
             for t in range(4):
                 mx1(pb[(c, b)][:, P * t : P * (t + 1)], LV, 512 + P * t, slice(lo, lo + P))
 
-        def evac_v(c, b):
+        def empty_v(c, b):
             if b == 0:
-                hp[c] = work.tile([P, CH, 4], BF16, tag="hp", name="hp", align_bytes=64)
+                hp[c] = work.tile([P, CHUNKS[c][1], 4], BF16, tag="hp", name="hp", align_bytes=64)
             nc.vector.tensor_tensor(
                 out=hp[c][:, P * b : P * (b + 1), :],
                 in0=pb[(c, b)][:].rearrange("p (t n) -> p n t", t=4),
@@ -253,29 +251,30 @@ def tile_infoncemi_pa_t_kernel(
             flat = hp[c][:].rearrange("p c t -> p (c t)")
             nc.vector.tensor_scalar(out=flat, in0=flat, scalar1=0.0, scalar2=None, op0=ALU.max)
 
-        def stage2(key, c, h, g):
+        def stage2(unit):
+            c, h, g = unit
             opens = (c, h) not in left
             if opens:
                 left[(c, h)] = 2
-                acc[(c, h)] = psum.tile([P, CH], F32, tag="acc%d" % h, name="acc")
+                acc[(c, h)] = psum.tile([P, CHUNKS[c][1]], F32, tag="acc%d" % h, name="acc")
             left[(c, h)] -= 1
             cols = slice(Y_DIM * g, Y_DIM * (g + 1))
             nc.tensor.matmul_mx(
                 out=acc[(c, h)][:],
                 lhsT=w2c[h][:, cols].bitcast(FP8X4),
                 lhsT_scale=w2s[h][:, cols],
-                rhs=hq[key][:].bitcast(FP8X4),
-                rhs_scale=hs[key][:],
+                rhs=hq[unit][:].bitcast(FP8X4),
+                rhs_scale=hs[unit][:],
                 start=opens,
                 stop=left[(c, h)] == 0,
             )
 
         def ep_tile(c, what):
-            ep[(c, what)] = work.tile([P, CH], F32, tag="ep_" + what, name="ep_" + what)
+            ep[(c, what)] = work.tile([P, CHUNKS[c][1]], F32, tag="ep_" + what, name="ep_" + what)
             return ep[(c, what)]
 
         def tanh_lv(c):
-            nc.scalar.activation(out=ep_tile(c, "th")[:], in_=acc[(c, LV)][:], func=ACT.Tanh, bias=bias_sb[:, 16:17])
+            nc.scalar.activation(out=ep_tile(c, "th")[:], in_=acc[(c, LV)][:], func=ACT.Tanh, bias=bias2_sb[:, 0:1])
 
         def exp_w(c):
             nc.scalar.activation(out=ep_tile(c, "w")[:], in_=ep[(c, "th")][:], func=ACT.Exp, scale=-1.0)
@@ -285,8 +284,8 @@ def tile_infoncemi_pa_t_kernel(
 
         def diff_d(c):
             nc.vector.scalar_tensor_tensor(
-                out=ep_tile(c, "d")[:], in0=acc[(c, MU)][:], scalar=bias_sb[:, 17:18],
-                in1=yT[:, CH * c : CH * (c + 1)], op0=ALU.add, op1=ALU.subtract,
+                out=ep_tile(c, "d")[:], in0=acc[(c, MU)][:], scalar=bias2_sb[:, 1:2],
+                in1=yT[:, cols_of(c)], op0=ALU.add, op1=ALU.subtract,
             )
 
         def sq_d(c):
@@ -304,23 +303,21 @@ def tile_infoncemi_pa_t_kernel(
         def term_p(c):
             nc.vector.tensor_tensor(out=ep_tile(c, "p")[:], in0=ep[(c, "d2")][:], in1=ep[(c, "w")][:], op=ALU.mult)
 
-        def term_p_on_vector(c):
-            nc.vector.tensor_tensor(out=ep_tile(c, "p")[:], in0=ep[(c, "d2")][:], in1=ep[(c, "w")][:], op=ALU.mult)
-
         def sums_over_d(c, what):
             o = 0 if what == "p" else 1
-            row = N_CH * o + c
+            row, col = divmod(CHUNKS[c][0], BANK)
+            row += N_ROWS * o
             if misc["sums"] == 0:
-                misc["r"] = psum.tile([P, CH], F32, tag="mr", name="r_ps")
+                misc["r"] = psum.tile([P, BANK], F32, tag="mr", name="r_ps")
             misc["sums"] += 1
             nc.tensor.matmul(
-                out=misc["r"][:], lhsT=sel[o][:, P - row : 2 * P - row], rhs=ep[(c, what)][:],
-                start=(misc["sums"] == 1), stop=(misc["sums"] == 2 * N_CH),
+                out=misc["r"][:, col : col + CHUNKS[c][1]], lhsT=sel[o][:, P - row : 2 * P - row], rhs=ep[(c, what)][:],
+                start=(misc["sums"] == 1), stop=(misc["sums"] == 2 * NC),
             )
 
         def gram(part):
             if part == 0:
-                misc["g"] = psum.tile([P, CH], F32, tag="mr", name="g_ps")
+                misc["g"] = psum.tile([P, BANK], F32, tag="mr", name="g_ps")
             for i in range(8):
                 j = 8 * part + i
                 nc.tensor.matmul(
@@ -336,133 +333,133 @@ def tile_infoncemi_pa_t_kernel(
                 out=stat[:, 1:2], in0=g_ps[:, P : P + 1], scalar1=inv_n, scalar2=None, op0=ALU.mult
             )
             nc.vector.reduce_sum(out=stat[:, 0:1], in_=gd[:], axis=AX.X)
-            nc.vector.tensor_tensor(out=stat[:, 2:3], in0=bias_sb[:, 17:18], in1=stat[:, 1:2], op=ALU.subtract)
+            nc.vector.tensor_tensor(out=stat[:, 2:3], in0=bias2_sb[:, 1:2], in1=stat[:, 1:2], op=ALU.subtract)
             nc.vector.tensor_tensor(out=stat[:, 3:4], in0=stat[:, 1:2], in1=stat[:, 1:2], op=ALU.mult)
             nc.vector.scalar_tensor_tensor(
                 out=stat[:, 4:5], in0=stat[:, 0:1], scalar=inv_n, in1=stat[:, 3:4], op0=ALU.mult, op1=ALU.subtract
             )
 
-        xt = {}
-        xg = {}
-
-        def x_first_evac(c, half):
-            if half == 0:
-                xg[c] = work.tile([P, 2 * CH], F32, tag="xg", name="xg", align_bytes=64)
-            x_evac(xg[c], half, xt.pop((c, half)))
-
-        for half in range(2):
-            xt[(0, half)] = x_transposes(0, half)
-            x_first_evac(0, half)
-        x_quant(0, xg[0])
-        bt_ps = side_bank([P, P], BF16, "bt_ps")
+        for half in range(CHUNKS[0][1] // 256):
+            fill(("x", 0, half))
+            empty(("x", 0, half))
+        bt_ps = psum.tile([P, P], BF16, tag="v", name="bt_ps")
         nc.tensor.transpose(bt_ps[:], braw[:], ident_b[:])
-        wg = w1_regroup(LV, 0)
-        nc.vector.tensor_copy(out=bias_sb[:], in_=bt_ps[:, 0:32])
-        w1_quant(LV, 0, wg)
-        wg = w1_regroup(LV, 1)
-        w1_quant(LV, 1, wg)
+        wg0 = w1_regroup(LV, 0, "v")
+        wg1 = w1_regroup(LV, 1, "s")
+        x_quant(0)
+        nc.vector.tensor_copy(out=bias_sb[:], in_=bt_ps[:, 0:16])
+        w1_quant(LV, 0, wg0)
 
-        def phase(k):
-            if k >= n_steps:
-                return N_CH, k - n_steps
-            if k < 0:
-                return -1, 0
-            return steps[k][0], k - first[steps[k][0]]
+        n_steps = 4 * NC
+        step_banks = []
+        regroup_at = {}
+        relu_at = {}
+        y_done = 0
+        for c in range(NC):
+            if c in V_CHUNKS:
+                units = [(c, LV, 0), (c, MU, 0), (c, MU, 1)]
+                offsets = (2, 3, 5)
+                relu_at[4 * c + 4] = c
+            else:
+                units = [(c, h, g) for h in range(2) for g in range(2)]
+                offsets = (1, 2, 3, 4)
+            for unit, offset in zip(units, offsets):
+                regroup_at.setdefault(4 * c + offset, []).append(unit)
+            banks_of_chunk = [("u", unit, t) for unit in units for t in range(4)]
+            n = len(units)
+            for r in range(4):
+                here = banks_of_chunk[n * r : n * (r + 1)]
+                if c + 1 < NC and r < CHUNKS[c + 1][1] // 256:
+                    here.append(("x", c + 1, r))
+                if r == 2 and c >= 1 and cols_of(c - 1).stop > P * y_done:
+                    here.append(("y", y_done, 0))
+                    y_done += 8
+                step_banks.append(here)
+        stream = [bank for here in step_banks for bank in here]
+        quant_at = {}
+        for s in list(regroup_at):
+            for unit in regroup_at[s]:
+                quant_at.setdefault(s + 1, []).append(unit)
+        for s in list(relu_at):
+            quant_at.setdefault(s + 1, []).append((relu_at[s], LV, 1))
 
-        last = N_CH - 1
+        done = 0
         for n in range(RING):
-            fill(*divmod(n, 4))
-        for k in range(n_steps + 2 + LAG):
-            c, i = phase(k)
-            kv = k - LAG
-            cv, iv = phase(kv)
-            prev = cv - 1
-            nxt = c + 1 if 0 <= c < last else None
-            x_step = 1 if c == 0 else 0
+            fill(stream[n])
+        for s in range(n_steps + 8):
+            c, r = divmod(s, 4)
+            old = c - 1
+            older = c - 2
+            ends = 0 <= older < NC
+            here = step_banks[s] if s < n_steps else []
 
-            for t in range(4):
-                if t == 0 and iv == 2 and 1 <= cv < N_CH:
-                    exp_w(prev)
-                if k < n_steps:
-                    evac(k, t)
-                if nxt and i == x_step and t >= 2:
-                    x_first_evac(nxt, t - 2)
-                if t == 2 and iv == 1 and cv >= 1:
-                    tanh_lv(prev)
-                if i == 1 and t == 1 and c % 2 == 1:
-                    nc.scalar.copy(out=yT[:, CH * (c - 1) : CH * (c + 1)], in_=misc["yt"][:])
-
-                ahead = 4 * k + t + RING
-                if ahead < 4 * n_steps:
-                    fill(*divmod(ahead, 4))
-                if nxt and i == x_step and t < 2:
-                    xt[(nxt, t)] = x_transposes(nxt, t)
-                if i == 0 and t == 3 and c % 2 == 1:
-                    misc["yt"] = y_transposes(c - 1)
-                if iv == 1 and t == 0 and has_v(prev):
-                    stage2(("v", prev), prev, LV, 1)
-                if t == 2 and 0 <= kv - 2 < n_steps:
-                    stage2(kv - 2, *steps[kv - 2])
-                if has_v(cv) and (iv, t) in V_FILLS:
-                    fill_v(cv, V_FILLS.index((iv, t)))
-                if cv >= 2 and iv == 0 and t == 3:
-                    sums_over_d(cv - 2, "p")
-                if cv >= 2 and iv == 1 and t == 1:
-                    sums_over_d(cv - 2, "q")
-                if k == 4:
-                    gram(t)
-
-            if nxt and i == x_step + 1 and not XQ_LATE:
-                x_quant(nxt, xg[nxt])
-            if 0 <= kv - 1 < n_steps:
-                regroup(kv - 1)
-            if k == 0:
-                wg = w1_regroup(MU, 0)
-                w1_quant(MU, 0, wg)
-            if k == 1:
-                wg = w1_regroup(MU, 1)
+            if s == 0:
+                wg2 = w1_regroup(MU, 0, "v")
+                w1_quant(LV, 1, wg1)
                 w2g = w2_regroup(LV)
-                w1_quant(MU, 1, wg)
+                w1_quant(MU, 0, wg2)
                 w2_quant(LV, w2g)
-            if k == 2:
+            if s == 1:
+                wg = w1_regroup(MU, 1, "v")
+            if r == 2 and c + 1 < NC:
+                x_quant(c + 1)
+            if r == 1 and ends:
+                term_q(older)
+            if r == 2 and ends:
+                term_p(older)
+            for unit in quant_at.get(s, []):
+                quant(unit)
+            if s in relu_at:
+                relu_v(relu_at[s])
+            for unit in regroup_at.get(s, []):
+                regroup(unit)
+            if s == 1:
+                w1_quant(MU, 1, wg)
+            if s == 2:
                 w2g = w2_regroup(MU)
-            if k == 5:
-                statistics()
-            if iv == 0 and cv >= 2:
-                term_q(cv - 2)
-            if iv == 0 and has_v(prev):
-                quant(("v", prev), hp[prev])
-            if iv == 2 and 1 <= cv < N_CH:
-                diff_d(prev)
-                sq_d(prev)
-                term_p(prev)
-            if iv in (1, 2) and has_v(cv):
-                for b in (2 * iv - 2, 2 * iv - 1):
-                    evac_v(cv, b)
-            if iv == 2 and has_v(cv):
-                relu_v(cv)
-            if 0 <= kv - 1 < n_steps:
-                quant(kv - 1, hg[kv - 1])
-            if k == 2:
+            if s == 3:
                 w2_quant(MU, w2g)
-            if nxt and i == x_step + 1 and XQ_LATE:
-                x_quant(nxt, xg[nxt])
+                b2_ps = psum.tile([P, P], BF16, tag="v", name="b2_ps")
+                nc.tensor.transpose(b2_ps[:], braw2[:], ident_b[:])
+                nc.vector.tensor_copy(out=bias2_sb[:], in_=b2_ps[:, 0:2])
+            if s == 7:
+                statistics()
 
-            if iv == 2 and 1 <= cv < N_CH:
-                sq_e(prev)
+            for i in range(max(4, len(here))):
+                if i == 1 and r == 3 and 0 <= old < NC:
+                    tanh_lv(old)
+                if i == 1 and r == 0 and ends:
+                    sq_e(older)
+                if i < len(here):
+                    empty(here[i])
+                    done += 1
+                    if done + RING <= len(stream):
+                        fill(stream[done + RING - 1])
+                if i == 0 and c in V_CHUNKS:
+                    fill_v(c, r)
+                if i == 1:
+                    for unit in quant_at.get(s - 1, []):
+                        stage2(unit)
+                if i == 2 and r == 2 and ends:
+                    sums_over_d(older, "q")
+                if i == 2 and r == 3 and ends:
+                    sums_over_d(older, "p")
+                if s in (5, 6) and i == 2:
+                    gram(2 * (s - 5))
+                    gram(2 * (s - 5) + 1)
+            if r == 3 and 0 <= old < NC:
+                exp_w(old)
+            if r == 1 and ends:
+                sq_d(older)
 
-        exp_w(last)
-        diff_d(last)
-        sq_e(last)
-        sq_d_on_vector(last)
-        term_p_on_vector(last)
-        sums_over_d(last, "p")
-        term_q(last)
-        sums_over_d(last, "q")
+            if r == 0 and ends:
+                diff_d(older)
+            if c in V_CHUNKS:
+                empty_v(c, r)
 
         nc.vector.tensor_copy(
             out=r_sb[:].rearrange("c (s j) -> c s j", j=4),
-            in_=misc["r"][0 : 2 * N_CH, :].rearrange("c (j s) -> c s j", j=4),
+            in_=misc["r"][0 : 2 * N_ROWS, :].rearrange("c (j s) -> c s j", j=4),
         )
-        nc.sync.dma_start(out=out_0.rearrange("(c i) -> c i", i=CH), in_=r_sb[0:N_CH, :])
-        nc.sync.dma_start(out=out_1.rearrange("(c i) -> c i", i=CH), in_=r_sb[N_CH : 2 * N_CH, :])
+        nc.sync.dma_start(out=out_0.rearrange("(c i) -> c i", i=BANK), in_=r_sb[0:N_ROWS, :])
+        nc.sync.dma_start(out=out_1.rearrange("(c i) -> c i", i=BANK), in_=r_sb[N_ROWS : 2 * N_ROWS, :])

@@ -24,7 +24,7 @@ Y_PITCH = 144
 LV, MU = 0, 1
 CHUNKS = [(BANK * c, BANK) for c in range(7)] + [(7 * BANK, 256), (7 * BANK + 256, 256)]
 NC = len(CHUNKS)
-V_CHUNKS = range(1, 7)
+V_CHUNKS = (1,2,3,4,5,6)
 RING = 4
 
 FLOPS = 2 * N_S * (2 * X_DIM * HID + 2 * HID * Y_DIM)
@@ -58,9 +58,8 @@ def tile_infoncemi_pa_t_kernel(
         y_sb = keep.tile([P, JT, Y_PITCH], BF16)
         yT = keep.tile([P, N_S], BF16)
         braw = keep.tile([P, P], BF16)
-        braw2 = keep.tile([P, P], BF16)
         bias_sb = keep.tile([P, 16], F32)
-        bias2_sb = keep.tile([P, 2], F32)
+        b2_sb = [keep.tile([P, 1], BF16, name="b2_%d" % h) for h in range(2)]
         ident_f = keep.tile([P, P], F32)
         ident_b = keep.tile([P, P], BF16)
         sel = [keep.tile([P, 2 * P], F32, name="sel%d" % o) for o in range(2)]
@@ -85,21 +84,20 @@ def tile_infoncemi_pa_t_kernel(
                 )
 
         nc.vector.memset(braw[:], 0.0)
+        load_w1(LV, 0)
         load_x(0, 2)
         load_x(2, 2)
-        load_w1(LV, 0)
         load_w1(LV, 1)
         for h in range(2):
             nc.scalar.dma_start(out=braw[8 * h : 8 * h + 8, :], in_=b1_dram[h].rearrange("(m p) -> m p", p=P))
         load_w1(MU, 0)
-        load_x(4, 4)
         load_w1(MU, 1)
+        load_x(4, 4)
         nc.vector.memset(y_sb[:, :, Y_DIM:Y_PITCH], 1.0)
-        nc.vector.memset(braw2[:], 0.0)
         for h in range(2):
             nc.sync.dma_start(out=w2raw[h][:], in_=w2_dram[h].rearrange("(m p) n -> p m n", p=P))
         for h in range(2):
-            nc.sync.dma_start(out=braw2[h : h + 1, :], in_=b2_dram[h].rearrange("(o p) -> o p", o=1))
+            nc.sync.dma_start(out=b2_sb[h][:], in_=b2_dram[h].rearrange("(p o) -> p o", o=1))
         for c in range(N_ROWS):
             nc.sync.dma_start(
                 out=y_sb[:, 4 * c : 4 * c + 4, 0:Y_DIM],
@@ -155,6 +153,7 @@ def tile_infoncemi_pa_t_kernel(
         ep = {}
         left = {}
         misc = {"ring": 0, "sums": 0}
+        w2g_of = {}
 
         def cols_of(c):
             return slice(CHUNKS[c][0], CHUNKS[c][0] + CHUNKS[c][1])
@@ -216,7 +215,7 @@ def tile_infoncemi_pa_t_kernel(
             )
 
         def regroup(unit):
-            hg[unit] = work.tile([P, CHUNKS[unit[0]][1], 4], BF16, tag="hg", name="hg", align_bytes=64)
+            hg[unit] = work.tile([P, CHUNKS[unit[0]][1], 4], BF16, tag="hg", name="hg", align_bytes=64, bufs=3)
             nc.vector.tensor_copy(
                 out=hg[unit][:].rearrange("p (c i) t -> p c t i", i=4),
                 in_=hc[unit][:].rearrange("p t (c i) -> p c t i", i=4),
@@ -274,7 +273,7 @@ def tile_infoncemi_pa_t_kernel(
             return ep[(c, what)]
 
         def tanh_lv(c):
-            nc.scalar.activation(out=ep_tile(c, "th")[:], in_=acc[(c, LV)][:], func=ACT.Tanh, bias=bias2_sb[:, 0:1])
+            nc.scalar.activation(out=ep_tile(c, "th")[:], in_=acc[(c, LV)][:], func=ACT.Tanh, bias=b2_sb[LV][:])
 
         def exp_w(c):
             nc.scalar.activation(out=ep_tile(c, "w")[:], in_=ep[(c, "th")][:], func=ACT.Exp, scale=-1.0)
@@ -284,7 +283,7 @@ def tile_infoncemi_pa_t_kernel(
 
         def diff_d(c):
             nc.vector.scalar_tensor_tensor(
-                out=ep_tile(c, "d")[:], in0=acc[(c, MU)][:], scalar=bias2_sb[:, 1:2],
+                out=ep_tile(c, "d")[:], in0=acc[(c, MU)][:], scalar=b2_sb[MU][:],
                 in1=yT[:, cols_of(c)], op0=ALU.add, op1=ALU.subtract,
             )
 
@@ -333,7 +332,7 @@ def tile_infoncemi_pa_t_kernel(
                 out=stat[:, 1:2], in0=g_ps[:, P : P + 1], scalar1=inv_n, scalar2=None, op0=ALU.mult
             )
             nc.vector.reduce_sum(out=stat[:, 0:1], in_=gd[:], axis=AX.X)
-            nc.vector.tensor_tensor(out=stat[:, 2:3], in0=bias2_sb[:, 1:2], in1=stat[:, 1:2], op=ALU.subtract)
+            nc.vector.tensor_tensor(out=stat[:, 2:3], in0=b2_sb[MU][:], in1=stat[:, 1:2], op=ALU.subtract)
             nc.vector.tensor_tensor(out=stat[:, 3:4], in0=stat[:, 1:2], in1=stat[:, 1:2], op=ALU.mult)
             nc.vector.scalar_tensor_tensor(
                 out=stat[:, 4:5], in0=stat[:, 0:1], scalar=inv_n, in1=stat[:, 3:4], op0=ALU.mult, op1=ALU.subtract
@@ -345,10 +344,10 @@ def tile_infoncemi_pa_t_kernel(
         bt_ps = psum.tile([P, P], BF16, tag="v", name="bt_ps")
         nc.tensor.transpose(bt_ps[:], braw[:], ident_b[:])
         wg0 = w1_regroup(LV, 0, "v")
-        wg1 = w1_regroup(LV, 1, "s")
-        x_quant(0)
-        nc.vector.tensor_copy(out=bias_sb[:], in_=bt_ps[:, 0:16])
         w1_quant(LV, 0, wg0)
+        nc.vector.tensor_copy(out=bias_sb[:], in_=bt_ps[:, 0:16])
+        x_quant(0)
+        wg1 = w1_regroup(LV, 1, "v")
 
         n_steps = 4 * NC
         step_banks = []
@@ -369,8 +368,8 @@ def tile_infoncemi_pa_t_kernel(
             n = len(units)
             for r in range(4):
                 here = banks_of_chunk[n * r : n * (r + 1)]
-                if c + 1 < NC and r < CHUNKS[c + 1][1] // 256:
-                    here.append(("x", c + 1, r))
+                if c + 1 < NC and r == 0:
+                    here += [("x", c + 1, half) for half in range(CHUNKS[c + 1][1] // 256)]
                 if r == 2 and c >= 1 and cols_of(c - 1).stop > P * y_done:
                     here.append(("y", y_done, 0))
                     y_done += 8
@@ -396,9 +395,7 @@ def tile_infoncemi_pa_t_kernel(
             if s == 0:
                 wg2 = w1_regroup(MU, 0, "v")
                 w1_quant(LV, 1, wg1)
-                w2g = w2_regroup(LV)
                 w1_quant(MU, 0, wg2)
-                w2_quant(LV, w2g)
             if s == 1:
                 wg = w1_regroup(MU, 1, "v")
             if r == 2 and c + 1 < NC:
@@ -415,13 +412,10 @@ def tile_infoncemi_pa_t_kernel(
                 regroup(unit)
             if s == 1:
                 w1_quant(MU, 1, wg)
-            if s == 2:
-                w2g = w2_regroup(MU)
-            if s == 3:
-                w2_quant(MU, w2g)
-                b2_ps = psum.tile([P, P], BF16, tag="v", name="b2_ps")
-                nc.tensor.transpose(b2_ps[:], braw2[:], ident_b[:])
-                nc.vector.tensor_copy(out=bias2_sb[:], in_=b2_ps[:, 0:2])
+            if s in (1, 2):
+                w2g_of[s - 1] = w2_regroup(s - 1)
+            if s in (2, 3):
+                w2_quant(s - 2, w2g_of[s - 2])
             if s == 7:
                 statistics()
 
@@ -435,7 +429,7 @@ def tile_infoncemi_pa_t_kernel(
                     done += 1
                     if done + RING <= len(stream):
                         fill(stream[done + RING - 1])
-                if i == 0 and c in V_CHUNKS:
+                if i == 0 and c in V_CHUNKS and P * r < CHUNKS[c][1]:
                     fill_v(c, r)
                 if i == 1:
                     for unit in quant_at.get(s - 1, []):
@@ -454,7 +448,7 @@ def tile_infoncemi_pa_t_kernel(
 
             if r == 0 and ends:
                 diff_d(older)
-            if c in V_CHUNKS:
+            if c in V_CHUNKS and P * r < CHUNKS[c][1]:
                 empty_v(c, r)
 
         nc.vector.tensor_copy(

@@ -240,9 +240,9 @@ def tile_infoncemi_pa_t_kernel(
             if b == 0:
                 hp[c] = work.tile([P, CHUNKS[c][1], 4], BF16, tag="hp", name="hp", align_bytes=64)
             nc.vector.tensor_tensor(
-                out=hp[c][:, P * b : P * (b + 1), :],
-                in0=pb[(c, b)][:].rearrange("p (t n) -> p n t", t=4),
-                in1=bias_sb[:, 4:8].unsqueeze(1).to_broadcast([P, P, 4]),
+                out=hp[c][:, P * b : P * (b + 1), :].rearrange("p (n i) t -> p n t i", i=4),
+                in0=pb[(c, b)][:].rearrange("p (t n i) -> p n t i", t=4, i=4),
+                in1=bias_sb[:, 4:8].unsqueeze(1).unsqueeze(3).to_broadcast([P, P // 4, 4, 4]),
                 op=ALU.add,
             )
 

@@ -24,7 +24,11 @@ Y_PITCH = 144
 LV, MU = 0, 1
 CHUNKS = [(BANK * c, BANK) for c in range(7)] + [(7 * BANK, 256), (7 * BANK + 256, 256)]
 NC = len(CHUNKS)
+X_OF = {c: CHUNKS[c] for c in range(NC)}
 V_CHUNKS = (1,2,3,4,5,6)
+B_STEPS = []
+SHARED = ((MU, 0),)
+S_COLS = 96
 RING = 4
 
 FLOPS = 2 * N_S * (2 * X_DIM * HID + 2 * HID * Y_DIM)
@@ -49,6 +53,7 @@ def tile_infoncemi_pa_t_kernel(
         x_sb = keep.tile([P, JT * X_DIM], BF16)
         xc = keep.tile([P, N_S], U32, align_bytes=64)
         xs = keep.tile([P, N_S], U8, align_bytes=64)
+        w1first = [keep.tile([P, 4, 256], BF16, name="w1first%d" % i) for i in range(2)]
         w1raw = [[keep.tile([P, 4, 512], BF16, name="w1raw%d%d" % (h, g)) for g in range(2)] for h in range(2)]
         w1c = [keep.tile([P, HID], U32, name="w1c%d" % h, align_bytes=64) for h in range(2)]
         w1s = [keep.tile([P, HID], U8, name="w1s%d" % h, align_bytes=64) for h in range(2)]
@@ -64,6 +69,7 @@ def tile_infoncemi_pa_t_kernel(
         ident_b = keep.tile([P, P], BF16)
         sel = [keep.tile([P, 2 * P], F32, name="sel%d" % o) for o in range(2)]
         stat = keep.tile([P, 8], F32)
+        stat2 = keep.tile([P, 32], F32)
         r_sb = keep.tile([2 * N_ROWS, BANK], F32)
         warm = keep.tile([P, 1], F32)
 
@@ -84,15 +90,24 @@ def tile_infoncemi_pa_t_kernel(
                 )
 
         nc.vector.memset(braw[:], 0.0)
-        load_w1(LV, 0)
         load_x(0, 2)
         load_x(2, 2)
+        for u in range(2):
+            nc.sync.dma_start(
+                out=w1first[0][:, 2 * u : 2 * u + 2, :],
+                in_=lv_W1[256 * u : 256 * (u + 1), 0 : 256].rearrange("(q e) c -> q e c", e=2),
+            )
+        for u in range(2):
+            nc.sync.dma_start(
+                out=w1first[1][:, 2 * u : 2 * u + 2, :],
+                in_=lv_W1[256 * u : 256 * (u + 1), 256 : 512].rearrange("(q e) c -> q e c", e=2),
+            )
         load_w1(LV, 1)
         for h in range(2):
             nc.scalar.dma_start(out=braw[8 * h : 8 * h + 8, :], in_=b1_dram[h].rearrange("(m p) -> m p", p=P))
         load_w1(MU, 0)
-        load_w1(MU, 1)
         load_x(4, 4)
+        load_w1(MU, 1)
         nc.vector.memset(y_sb[:, :, Y_DIM:Y_PITCH], 1.0)
         for h in range(2):
             nc.sync.dma_start(out=w2raw[h][:], in_=w2_dram[h].rearrange("(m p) n -> p m n", p=P))
@@ -181,12 +196,15 @@ def tile_infoncemi_pa_t_kernel(
             elif kind == "x":
                 banks[item] = psum.tile([P, BANK], F32, tag=tag, name="bank")
                 for n in range(4):
-                    lo = 2 * CHUNKS[key][0] + 512 * t + P * n
+                    lo = 2 * X_OF[key][0] + 512 * t + P * n
                     nc.tensor.transpose(banks[item][:, P * n : P * (n + 1)], x_words[:, lo : lo + P], ident_f[:])
             else:
-                banks[item] = psum.tile([P, 8 * P], BF16, tag=tag, name="bank")
-                for n in range(8):
-                    nc.tensor.transpose(banks[item][:, P * n : P * (n + 1)], y_sb[:, key + n, 0:Y_DIM], ident_b[:])
+                lo, width = CHUNKS[key]
+                banks[item] = psum.tile([P, width], BF16, tag=tag, name="bank")
+                for n in range(width // P):
+                    nc.tensor.transpose(
+                        banks[item][:, P * n : P * (n + 1)], y_sb[:, lo // P + n, 0:Y_DIM], ident_b[:]
+                    )
 
         def empty(item):
             kind, key, t = item
@@ -201,24 +219,36 @@ def tile_infoncemi_pa_t_kernel(
                 )
             elif kind == "x":
                 if t == 0:
-                    xg[key] = work.tile([P, 2 * CHUNKS[key][1]], F32, tag="xg", name="xg", align_bytes=64)
+                    xg[key] = work.tile([P, 2 * X_OF[key][1]], F32, tag="xg", name="xg", align_bytes=64)
                 nc.scalar.copy(
                     out=xg[key][:, BANK * t : BANK * (t + 1)].rearrange("q (j s u) -> q j s u", j=2, u=2),
                     in_=bank[:].rearrange("q (j u s) -> q j s u", j=2, u=2),
                 )
             else:
-                nc.scalar.copy(out=yT[:, P * key : P * (key + 8)], in_=bank[:])
+                nc.scalar.copy(out=yT[:, cols_of(key)], in_=bank[:])
 
         def x_quant(c):
-            nc.vector.quantize_mx(
-                out=xc[:, cols_of(c)].bitcast(FP8X4), scales=xs[:, cols_of(c)], in_=xg[c][:].bitcast(BF16)
-            )
+            cols = slice(X_OF[c][0], X_OF[c][0] + X_OF[c][1])
+            nc.vector.quantize_mx(out=xc[:, cols].bitcast(FP8X4), scales=xs[:, cols], in_=xg[c][:].bitcast(BF16))
+
+        def shared(unit):
+            return unit[0] in V_CHUNKS and unit[1:] in SHARED
 
         def regroup(unit):
-            hg[unit] = work.tile([P, CHUNKS[unit[0]][1], 4], BF16, tag="hg", name="hg", align_bytes=64, bufs=3)
+            width = CHUNKS[unit[0]][1] - (S_COLS if shared(unit) else 0)
+            if unit not in hg:
+                hg[unit] = work.tile([P, CHUNKS[unit[0]][1], 4], BF16, tag="hg", name="hg", align_bytes=64, bufs=4)
             nc.vector.tensor_copy(
-                out=hg[unit][:].rearrange("p (c i) t -> p c t i", i=4),
-                in_=hc[unit][:].rearrange("p t (c i) -> p c t i", i=4),
+                out=hg[unit][:, 0:width, :].rearrange("p (c i) t -> p c t i", i=4),
+                in_=hc[unit][:, :, 0:width].rearrange("p t (c i) -> p c t i", i=4),
+            )
+
+        def regroup_on_scalar(unit):
+            width = CHUNKS[unit[0]][1]
+            hg[unit] = work.tile([P, width, 4], BF16, tag="hg", name="hg", align_bytes=64, bufs=4)
+            nc.scalar.copy(
+                out=hg[unit][:, width - S_COLS : width, :].rearrange("p (c i) t -> p c t i", i=4),
+                in_=hc[unit][:, :, width - S_COLS : width].rearrange("p t (c i) -> p c t i", i=4),
             )
 
         def quant(unit):
@@ -244,6 +274,19 @@ def tile_infoncemi_pa_t_kernel(
                 in0=pb[(c, b)][:].rearrange("p (t n i) -> p n t i", t=4, i=4),
                 in1=bias_sb[:, 4:8].unsqueeze(1).unsqueeze(3).to_broadcast([P, P // 4, 4, 4]),
                 op=ALU.add,
+            )
+
+        def fill_b(unit):
+            c, h, g = unit
+            pb[unit] = psum.tile([P, CHUNKS[c][1]], F32, tag="v", name="pb")
+            mx1(pb[unit][:], h, 512 * g + 3 * P, cols_of(c))
+
+        def empty_b(unit):
+            c, h, g = unit
+            col = 8 * h + 4 * g + 3
+            nc.vector.tensor_scalar(
+                out=hc[unit][:, 3, :], in0=pb[unit][:], scalar1=bias_sb[:, col : col + 1], scalar2=0.0,
+                op0=ALU.add, op1=ALU.max,
             )
 
         def relu_v(c):
@@ -279,7 +322,7 @@ def tile_infoncemi_pa_t_kernel(
             nc.scalar.activation(out=ep_tile(c, "w")[:], in_=ep[(c, "th")][:], func=ACT.Exp, scale=-1.0)
 
         def sq_e(c):
-            nc.scalar.activation(out=ep_tile(c, "e2")[:], in_=acc[(c, MU)][:], func=ACT.Square, bias=stat[:, 2:3])
+            nc.scalar.activation(out=ep_tile(c, "e2")[:], in_=acc[(c, MU)][:], func=ACT.Square, bias=stat2[:, 0:1])
 
         def diff_d(c):
             nc.vector.scalar_tensor_tensor(
@@ -295,7 +338,7 @@ def tile_infoncemi_pa_t_kernel(
 
         def term_q(c):
             nc.vector.scalar_tensor_tensor(
-                out=ep_tile(c, "q")[:], in0=ep[(c, "e2")][:], scalar=stat[:, 4:5], in1=ep[(c, "w")][:],
+                out=ep_tile(c, "q")[:], in0=ep[(c, "e2")][:], scalar=stat2[:, 24:25], in1=ep[(c, "w")][:],
                 op0=ALU.add, op1=ALU.mult,
             )
 
@@ -332,28 +375,40 @@ def tile_infoncemi_pa_t_kernel(
                 out=stat[:, 1:2], in0=g_ps[:, P : P + 1], scalar1=inv_n, scalar2=None, op0=ALU.mult
             )
             nc.vector.reduce_sum(out=stat[:, 0:1], in_=gd[:], axis=AX.X)
-            nc.vector.tensor_tensor(out=stat[:, 2:3], in0=b2_sb[MU][:], in1=stat[:, 1:2], op=ALU.subtract)
-            nc.vector.tensor_tensor(out=stat[:, 3:4], in0=stat[:, 1:2], in1=stat[:, 1:2], op=ALU.mult)
-            nc.vector.scalar_tensor_tensor(
-                out=stat[:, 4:5], in0=stat[:, 0:1], scalar=inv_n, in1=stat[:, 3:4], op0=ALU.mult, op1=ALU.subtract
-            )
+            nc.gpsimd.tensor_tensor(out=stat2[:, 0:1], in0=b2_sb[MU][:], in1=stat[:, 1:2], op=ALU.subtract)
+            nc.gpsimd.tensor_tensor(out=stat2[:, 8:9], in0=stat[:, 1:2], in1=stat[:, 1:2], op=ALU.mult)
+            nc.gpsimd.tensor_scalar(out=stat2[:, 16:17], in0=stat[:, 0:1], scalar1=inv_n, scalar2=None, op0=ALU.mult)
+            nc.gpsimd.tensor_tensor(out=stat2[:, 24:25], in0=stat2[:, 16:17], in1=stat2[:, 8:9], op=ALU.subtract)
 
         for half in range(CHUNKS[0][1] // 256):
             fill(("x", 0, half))
             empty(("x", 0, half))
         bt_ps = psum.tile([P, P], BF16, tag="v", name="bt_ps")
         nc.tensor.transpose(bt_ps[:], braw[:], ident_b[:])
-        wg0 = w1_regroup(LV, 0, "v")
-        w1_quant(LV, 0, wg0)
+        wgf0 = work.tile([P, 256, 4], BF16, tag="wgf", name="wgf0", align_bytes=64)
+        nc.vector.tensor_copy(
+            out=wgf0[:].rearrange("p (c i) t -> p c t i", i=4), in_=w1first[0][:].rearrange("p t (c i) -> p c t i", i=4)
+        )
+        wgf1 = work.tile([P, 256, 4], BF16, tag="wgf", name="wgf1", align_bytes=64)
+        nc.vector.tensor_copy(
+            out=wgf1[:].rearrange("p (c i) t -> p c t i", i=4), in_=w1first[1][:].rearrange("p t (c i) -> p c t i", i=4)
+        )
+        nc.vector.quantize_mx(
+            out=w1c[LV][:, 0 : 256].bitcast(FP8X4), scales=w1s[LV][:, 0 : 256],
+            in_=wgf0[:].rearrange("p c t -> p (c t)"),
+        )
         nc.vector.tensor_copy(out=bias_sb[:], in_=bt_ps[:, 0:16])
         x_quant(0)
+        nc.vector.quantize_mx(
+            out=w1c[LV][:, 256 : 512].bitcast(FP8X4), scales=w1s[LV][:, 256 : 512],
+            in_=wgf1[:].rearrange("p c t -> p (c t)"),
+        )
         wg1 = w1_regroup(LV, 1, "v")
 
         n_steps = 4 * NC
         step_banks = []
         regroup_at = {}
         relu_at = {}
-        y_done = 0
         for c in range(NC):
             if c in V_CHUNKS:
                 units = [(c, LV, 0), (c, MU, 0), (c, MU, 1)]
@@ -368,11 +423,14 @@ def tile_infoncemi_pa_t_kernel(
             n = len(units)
             for r in range(4):
                 here = banks_of_chunk[n * r : n * (r + 1)]
-                if c + 1 < NC and r == 0:
-                    here += [("x", c + 1, half) for half in range(CHUNKS[c + 1][1] // 256)]
-                if r == 2 and c >= 1 and cols_of(c - 1).stop > P * y_done:
-                    here.append(("y", y_done, 0))
-                    y_done += 8
+                if (c, r) in B_STEPS:
+                    here.pop()
+                if c + 1 in X_OF and r == 0:
+                    here += [("x", c + 1, half) for half in range(X_OF[c + 1][1] // 256)]
+                if r == 2 and c >= 1:
+                    here.append(("y", c - 1, 0))
+                if r == 3 and c == NC - 1:
+                    here.append(("y", c, 0))
                 step_banks.append(here)
         stream = [bank for here in step_banks for bank in here]
         quant_at = {}
@@ -398,11 +456,11 @@ def tile_infoncemi_pa_t_kernel(
                 w1_quant(MU, 0, wg2)
             if s == 1:
                 wg = w1_regroup(MU, 1, "v")
-            if r == 2 and c + 1 < NC:
+            if r == 2 and c + 1 in X_OF:
                 x_quant(c + 1)
             if r == 1 and ends:
                 term_q(older)
-            if r == 2 and ends:
+            if r == 3 and ends:
                 term_p(older)
             for unit in quant_at.get(s, []):
                 quant(unit)
@@ -422,7 +480,7 @@ def tile_infoncemi_pa_t_kernel(
             for i in range(max(4, len(here))):
                 if i == 1 and r == 3 and 0 <= old < NC:
                     tanh_lv(old)
-                if i == 1 and r == 0 and ends:
+                if i == 2 and r == 0 and ends:
                     sq_e(older)
                 if i < len(here):
                     empty(here[i])
@@ -431,16 +489,21 @@ def tile_infoncemi_pa_t_kernel(
                         fill(stream[done + RING - 1])
                 if i == 0 and c in V_CHUNKS and P * r < CHUNKS[c][1]:
                     fill_v(c, r)
+                if i == 1 and (c, r) in B_STEPS:
+                    fill_b((c, r // 2, r % 2))
                 if i == 1:
                     for unit in quant_at.get(s - 1, []):
                         stage2(unit)
-                if i == 2 and r == 2 and ends:
+                if i == 3 and r == 2 and ends:
                     sums_over_d(older, "q")
-                if i == 2 and r == 3 and ends:
+                if i == 3 and r == 3 and ends:
                     sums_over_d(older, "p")
                 if s in (5, 6) and i == 2:
                     gram(2 * (s - 5))
                     gram(2 * (s - 5) + 1)
+            for item in here:
+                if item[0] == "u" and item[2] == 3 and shared(item[1]):
+                    regroup_on_scalar(item[1])
             if r == 3 and 0 <= old < NC:
                 exp_w(old)
             if r == 1 and ends:
@@ -450,6 +513,8 @@ def tile_infoncemi_pa_t_kernel(
                 diff_d(older)
             if c in V_CHUNKS and P * r < CHUNKS[c][1]:
                 empty_v(c, r)
+            if (c, r) in B_STEPS:
+                empty_b((c, r // 2, r % 2))
 
         nc.vector.tensor_copy(
             out=r_sb[:].rearrange("c (s j) -> c s j", j=4),

@@ -29,6 +29,7 @@ V_CHUNKS = (1,2,3,4,5,6)
 B_STEPS = []
 SHARED = ((MU, 0),)
 S_COLS = 96
+HALVED = (6,)
 RING = 4
 
 FLOPS = 2 * N_S * (2 * X_DIM * HID + 2 * HID * Y_DIM)
@@ -345,16 +346,18 @@ def tile_infoncemi_pa_t_kernel(
         def term_p(c):
             nc.vector.tensor_tensor(out=ep_tile(c, "p")[:], in0=ep[(c, "d2")][:], in1=ep[(c, "w")][:], op=ALU.mult)
 
-        def sums_over_d(c, what):
+        def sums_over_d(c, what, cols=None):
             o = 0 if what == "p" else 1
             row, col = divmod(CHUNKS[c][0], BANK)
             row += N_ROWS * o
             if misc["sums"] == 0:
                 misc["r"] = psum.tile([P, BANK], F32, tag="mr", name="r_ps")
-            misc["sums"] += 1
+            cols = cols or slice(0, CHUNKS[c][1])
+            misc["sums"] += cols.stop - cols.start
             nc.tensor.matmul(
-                out=misc["r"][:, col : col + CHUNKS[c][1]], lhsT=sel[o][:, P - row : 2 * P - row], rhs=ep[(c, what)][:],
-                start=(misc["sums"] == 1), stop=(misc["sums"] == 2 * NC),
+                out=misc["r"][:, col + cols.start : col + cols.stop], lhsT=sel[o][:, P - row : 2 * P - row],
+                rhs=ep[(c, what)][:, cols],
+                start=(misc["sums"] == cols.stop - cols.start), stop=(misc["sums"] == 2 * N_S),
             )
 
         def gram(part):
@@ -385,6 +388,9 @@ def tile_infoncemi_pa_t_kernel(
             empty(("x", 0, half))
         bt_ps = psum.tile([P, P], BF16, tag="v", name="bt_ps")
         nc.tensor.transpose(bt_ps[:], braw[:], ident_b[:])
+        warm_ps = psum.tile([P, BANK], F32, tag="mr", name="warm_ps")
+        for n in range(3):
+            nc.tensor.matmul(out=warm_ps[:], lhsT=ident_b[:], rhs=x_sb[:, 0:BANK], start=True, stop=True)
         wgf0 = work.tile([P, 256, 4], BF16, tag="wgf", name="wgf0", align_bytes=64)
         nc.vector.tensor_copy(
             out=wgf0[:].rearrange("p (c i) t -> p c t i", i=4), in_=w1first[0][:].rearrange("p t (c i) -> p c t i", i=4)
@@ -450,6 +456,9 @@ def tile_infoncemi_pa_t_kernel(
             ends = 0 <= older < NC
             here = step_banks[s] if s < n_steps else []
 
+            if r == 0 and ends and c >= NC:
+                diff_d(older)
+                sq_e(older)
             if s == 0:
                 wg2 = w1_regroup(MU, 0, "v")
                 w1_quant(LV, 1, wg1)
@@ -480,7 +489,7 @@ def tile_infoncemi_pa_t_kernel(
             for i in range(max(4, len(here))):
                 if i == 1 and r == 3 and 0 <= old < NC:
                     tanh_lv(old)
-                if i == 2 and r == 0 and ends:
+                if i == 2 and r == 0 and ends and c < NC:
                     sq_e(older)
                 if i < len(here):
                     empty(here[i])
@@ -494,10 +503,18 @@ def tile_infoncemi_pa_t_kernel(
                 if i == 1:
                     for unit in quant_at.get(s - 1, []):
                         stage2(unit)
-                if i == 3 and r == 2 and ends:
+                if i == 3 and r == 2 and ends and older not in HALVED:
                     sums_over_d(older, "q")
-                if i == 3 and r == 3 and ends:
+                if i == 3 and r == 1 and ends and older in HALVED:
+                    sums_over_d(older, "q", slice(0 * 256, 0 * 256 + 256))
+                if i == 2 and r == 2 and ends and older in HALVED:
+                    sums_over_d(older, "q", slice(1 * 256, 1 * 256 + 256))
+                if i == 3 and r == 3 and ends and older not in HALVED:
                     sums_over_d(older, "p")
+                if i == 1 and r == 3 and ends and older in HALVED:
+                    sums_over_d(older, "p", slice(0 * 256, 0 * 256 + 256))
+                if i == 3 and r == 3 and ends and older in HALVED:
+                    sums_over_d(older, "p", slice(1 * 256, 1 * 256 + 256))
                 if s in (5, 6) and i == 2:
                     gram(2 * (s - 5))
                     gram(2 * (s - 5) + 1)
@@ -509,7 +526,7 @@ def tile_infoncemi_pa_t_kernel(
             if r == 1 and ends:
                 sq_d(older)
 
-            if r == 0 and ends:
+            if r == 0 and ends and c < NC:
                 diff_d(older)
             if c in V_CHUNKS and P * r < CHUNKS[c][1]:
                 empty_v(c, r)

@@ -133,8 +133,8 @@ def tile_infoncemi_pa_t_kernel(
 
         def w1_regroup(h, g, engine):
             wg = work.tile([P, 512, 4], BF16, tag="wg", name="wg", align_bytes=64, bufs=2)
-            dst = wg[:].rearrange("p (c i) t -> p c t i", i=4)
-            src = w1raw[h][g][:].rearrange("p t (c i) -> p c t i", i=4)
+            dst = wg[:].rearrange("p (c i) t -> p c t i", i=8)
+            src = w1raw[h][g][:].rearrange("p t (c i) -> p c t i", i=8)
             if engine == "s":
                 nc.scalar.copy(out=dst, in_=src)
             else:
@@ -240,16 +240,16 @@ def tile_infoncemi_pa_t_kernel(
             if unit not in hg:
                 hg[unit] = work.tile([P, CHUNKS[unit[0]][1], 4], BF16, tag="hg", name="hg", align_bytes=64, bufs=4)
             nc.vector.tensor_copy(
-                out=hg[unit][:, 0:width, :].rearrange("p (c i) t -> p c t i", i=4),
-                in_=hc[unit][:, :, 0:width].rearrange("p t (c i) -> p c t i", i=4),
+                out=hg[unit][:, 0:width, :].rearrange("p (c i) t -> p c t i", i=8),
+                in_=hc[unit][:, :, 0:width].rearrange("p t (c i) -> p c t i", i=8),
             )
 
         def regroup_on_scalar(unit):
             width = CHUNKS[unit[0]][1]
             hg[unit] = work.tile([P, width, 4], BF16, tag="hg", name="hg", align_bytes=64, bufs=4)
             nc.scalar.copy(
-                out=hg[unit][:, width - S_COLS : width, :].rearrange("p (c i) t -> p c t i", i=4),
-                in_=hc[unit][:, :, width - S_COLS : width].rearrange("p t (c i) -> p c t i", i=4),
+                out=hg[unit][:, width - S_COLS : width, :].rearrange("p (c i) t -> p c t i", i=8),
+                in_=hc[unit][:, :, width - S_COLS : width].rearrange("p t (c i) -> p c t i", i=8),
             )
 
         def quant(unit):
@@ -393,11 +393,11 @@ def tile_infoncemi_pa_t_kernel(
             nc.tensor.matmul(out=warm_ps[:], lhsT=ident_b[:], rhs=x_sb[:, 0:BANK], start=True, stop=True)
         wgf0 = work.tile([P, 256, 4], BF16, tag="wgf", name="wgf0", align_bytes=64)
         nc.vector.tensor_copy(
-            out=wgf0[:].rearrange("p (c i) t -> p c t i", i=4), in_=w1first[0][:].rearrange("p t (c i) -> p c t i", i=4)
+            out=wgf0[:].rearrange("p (c i) t -> p c t i", i=8), in_=w1first[0][:].rearrange("p t (c i) -> p c t i", i=8)
         )
         wgf1 = work.tile([P, 256, 4], BF16, tag="wgf", name="wgf1", align_bytes=64)
         nc.vector.tensor_copy(
-            out=wgf1[:].rearrange("p (c i) t -> p c t i", i=4), in_=w1first[1][:].rearrange("p t (c i) -> p c t i", i=4)
+            out=wgf1[:].rearrange("p (c i) t -> p c t i", i=8), in_=w1first[1][:].rearrange("p t (c i) -> p c t i", i=8)
         )
         nc.vector.quantize_mx(
             out=w1c[LV][:, 0 : 256].bitcast(FP8X4), scales=w1s[LV][:, 0 : 256],

from contextlib import ExitStack

import concourse.mybir as mybir
from concourse.masks import make_identity

F32 = mybir.dt.float32
BF16 = mybir.dt.bfloat16
U32 = mybir.dt.uint32
U8 = mybir.dt.uint8
FP8X4 = mybir.dt.float8_e4m3fn_x4
ACT = mybir.ActivationFunctionType
ALU = mybir.AluOpType
AX = mybir.AxisListType

P = 128
N_S = 4096
X_DIM = 512
HID = 1024
Y_DIM = 128
BANK = 512
JT = N_S // P
N_ROWS = N_S // BANK
Y_PITCH = 144
LV, MU = 0, 1
CHUNKS = [(BANK * c, BANK) for c in range(7)] + [(7 * BANK, 256), (7 * BANK + 256, 256)]
NC = len(CHUNKS)
X_OF = {c: CHUNKS[c] for c in range(NC)}
V_CHUNKS = (1,2,3,4,5,6)
B_STEPS = []
SHARED = ((MU, 0),)
S_COLS = 96
HALVED = (6,)
RING = 4

FLOPS = 2 * N_S * (2 * X_DIM * HID + 2 * HID * Y_DIM)


def tile_infoncemi_pa_t_kernel(
    tc, x_samples, y_samples, mu_W1, mu_b1, mu_W2, mu_b2, lv_W1, lv_b1, lv_W2, lv_b2, out_0, out_1
):
    nc = tc.nc
    w1_dram = (lv_W1, mu_W1)
    b1_dram = (lv_b1, mu_b1)
    w2_dram = (lv_W2, mu_W2)
    b2_dram = (lv_b2, mu_b2)
    inv_n = 1.0 / N_S

    with ExitStack() as ctx:
        keep = ctx.enter_context(tc.tile_pool(name="keep", bufs=1))
        work = ctx.enter_context(tc.tile_pool(name="work", bufs=2))
        psum = ctx.enter_context(tc.psum_pool(name="psum", bufs=1))
        ctx.enter_context(tc.manual_schedule())

        x_sb = keep.tile([P, JT * X_DIM], BF16)
        xc = keep.tile([P, N_S], U32, align_bytes=64)
        xs = keep.tile([P, N_S], U8, align_bytes=64)
        w1first = [keep.tile([P, 4, 256], BF16, name="w1first%d" % i) for i in range(2)]
        w1raw = [[keep.tile([P, 4, 512], BF16, name="w1raw%d%d" % (h, g)) for g in range(2)] for h in range(2)]
        w1c = [keep.tile([P, HID], U32, name="w1c%d" % h, align_bytes=64) for h in range(2)]
        w1s = [keep.tile([P, HID], U8, name="w1s%d" % h, align_bytes=64) for h in range(2)]
        w2raw = [keep.tile([P, 8, Y_DIM], BF16, name="w2raw%d" % h) for h in range(2)]
        w2c = [keep.tile([P, 2 * Y_DIM], U32, name="w2c%d" % h, align_bytes=64) for h in range(2)]
        w2s = [keep.tile([P, 2 * Y_DIM], U8, name="w2s%d" % h, align_bytes=64) for h in range(2)]
        y_sb = keep.tile([P, JT, Y_PITCH], BF16)
        yT = keep.tile([P, N_S], BF16)
        braw = keep.tile([P, P], BF16)
        bias_sb = keep.tile([P, 16], F32)
        b2_sb = [keep.tile([P, 1], BF16, name="b2_%d" % h) for h in range(2)]
        ident_f = keep.tile([P, P], F32)
        ident_b = keep.tile([P, P], BF16)
        sel = [keep.tile([P, 2 * P], F32, name="sel%d" % o) for o in range(2)]
        stat = keep.tile([P, 8], F32)
        stat2 = keep.tile([P, 32], F32)
        r_sb = keep.tile([2 * N_ROWS, BANK], F32)
        warm = keep.tile([P, 1], F32)

        def load_x(first_tile, n_tiles):
            c, j = divmod(first_tile, 4)
            rows = x_samples[BANK * c : BANK * (c + 1), :].rearrange("(p j) k -> p (j k)", j=4)
            nc.sync.dma_start(
                out=x_sb[:, X_DIM * first_tile : X_DIM * (first_tile + n_tiles)],
                in_=rows[:, X_DIM * j : X_DIM * (j + n_tiles)],
            )

        def load_w1(h, g):
            cols = slice(512 * g, 512 * (g + 1))
            for u in range(2):
                nc.sync.dma_start(
                    out=w1raw[h][g][:, 2 * u : 2 * u + 2, :],
                    in_=w1_dram[h][256 * u : 256 * (u + 1), cols].rearrange("(q e) c -> q e c", e=2),
                )

        nc.vector.memset(braw[:], 0.0)
        load_x(0, 2)
        load_x(2, 2)
        for u in range(2):
            nc.sync.dma_start(
                out=w1first[0][:, 2 * u : 2 * u + 2, :],
                in_=lv_W1[256 * u : 256 * (u + 1), 0 : 256].rearrange("(q e) c -> q e c", e=2),
            )
        for u in range(2):
            nc.sync.dma_start(
                out=w1first[1][:, 2 * u : 2 * u + 2, :],
                in_=lv_W1[256 * u : 256 * (u + 1), 256 : 512].rearrange("(q e) c -> q e c", e=2),
            )
        load_w1(LV, 1)
        for h in range(2):
            nc.scalar.dma_start(out=braw[8 * h : 8 * h + 8, :], in_=b1_dram[h].rearrange("(m p) -> m p", p=P))
        load_w1(MU, 0)
        load_x(4, 4)
        load_w1(MU, 1)
        nc.vector.memset(y_sb[:, :, Y_DIM:Y_PITCH], 1.0)
        for h in range(2):
            nc.sync.dma_start(out=w2raw[h][:], in_=w2_dram[h].rearrange("(m p) n -> p m n", p=P))
        for h in range(2):
            nc.sync.dma_start(out=b2_sb[h][:], in_=b2_dram[h].rearrange("(p o) -> p o", o=1))
        for c in range(N_ROWS):
            nc.sync.dma_start(
                out=y_sb[:, 4 * c : 4 * c + 4, 0:Y_DIM],
                in_=y_samples[BANK * c : BANK * (c + 1), :].rearrange("(p j) d -> p j d", j=4),
            )
        for c in range(2, N_ROWS):
            load_x(4 * c, 4)

        make_identity(nc, ident_f[:])
        make_identity(nc, ident_b[:])
        for o in range(2):
            nc.gpsimd.memset(sel[o][:], 0.0)
            nc.gpsimd.memset(sel[o][:, P : P + 1], -0.5 * (1.0, inv_n)[o])
        nc.scalar.activation(out=warm[:], in_=ident_f[:, 0:1], func=ACT.Exp)

        x_words = x_sb[:].bitcast(F32)

        def w1_regroup(h, g, engine):
            wg = work.tile([P, 512, 4], BF16, tag="wg", name="wg", align_bytes=64, bufs=2)
            dst = wg[:].rearrange("p (c i) t -> p c t i", i=8)
            src = w1raw[h][g][:].rearrange("p t (c i) -> p c t i", i=8)
            if engine == "s":
                nc.scalar.copy(out=dst, in_=src)
            else:
                nc.vector.tensor_copy(out=dst, in_=src)
            return wg

        def w1_quant(h, g, wg):
            cols = slice(512 * g, 512 * (g + 1))
            nc.vector.quantize_mx(
                out=w1c[h][:, cols].bitcast(FP8X4), scales=w1s[h][:, cols], in_=wg[:].rearrange("p c t -> p (c t)")
            )

        def w2_regroup(h):
            w2g = work.tile([P, 2, Y_DIM, 4], BF16, tag="w2g", name="w2g", align_bytes=64)
            nc.vector.tensor_copy(out=w2g[:], in_=w2raw[h][:].rearrange("p (g t) n -> p g n t", t=4))
            return w2g

        def w2_quant(h, w2g):
            nc.vector.quantize_mx(
                out=w2c[h][:].bitcast(FP8X4), scales=w2s[h][:], in_=w2g[:].rearrange("p g n t -> p (g n t)")
            )

        banks = {}
        xg = {}
        hc = {}
        hg = {}
        hq = {}
        hs = {}
        hp = {}
        pb = {}
        acc = {}
        ep = {}
        left = {}
        misc = {"ring": 0, "sums": 0}
        w2g_of = {}

        def cols_of(c):
            return slice(CHUNKS[c][0], CHUNKS[c][0] + CHUNKS[c][1])

        def mx1(out, h, col, xcols):
            wcols = slice(col, col + P)
            nc.tensor.matmul_mx(
                out=out,
                lhsT=w1c[h][:, wcols].bitcast(FP8X4),
                lhsT_scale=w1s[h][:, wcols],
                rhs=xc[:, xcols].bitcast(FP8X4),
                rhs_scale=xs[:, xcols],
                start=True,
                stop=True,
            )

        def fill(item):
            kind, key, t = item
            misc["ring"] += 1
            tag = "s%d" % (misc["ring"] % RING)
            if kind == "u":
                c, h, g = key
                banks[item] = psum.tile([P, CHUNKS[c][1]], F32, tag=tag, name="bank")
                mx1(banks[item][:], h, 512 * g + P * t, cols_of(c))
            elif kind == "x":
                banks[item] = psum.tile([P, BANK], F32, tag=tag, name="bank")
                for n in range(4):
                    lo = 2 * X_OF[key][0] + 512 * t + P * n
                    nc.tensor.transpose(banks[item][:, P * n : P * (n + 1)], x_words[:, lo : lo + P], ident_f[:])
            else:
                lo, width = CHUNKS[key]
                banks[item] = psum.tile([P, width], BF16, tag=tag, name="bank")
                for n in range(width // P):
                    nc.tensor.transpose(
                        banks[item][:, P * n : P * (n + 1)], y_sb[:, lo // P + n, 0:Y_DIM], ident_b[:]
                    )

        def empty(item):
            kind, key, t = item
            bank = banks.pop(item)
            if kind == "u":
                c, h, g = key
                if t == 0:
                    hc[key] = work.tile([P, 4, CHUNKS[c][1]], BF16, tag="hc", name="hc", bufs=4)
                col = 8 * h + 4 * g + t
                nc.scalar.activation(
                    out=hc[key][:, t, :], in_=bank[:], func=ACT.Relu, bias=bias_sb[:, col : col + 1]
                )
            elif kind == "x":
                if t == 0:
                    xg[key] = work.tile([P, 2 * X_OF[key][1]], F32, tag="xg", name="xg", align_bytes=64)
                nc.scalar.copy(
                    out=xg[key][:, BANK * t : BANK * (t + 1)].rearrange("q (j s u) -> q j s u", j=2, u=2),
                    in_=bank[:].rearrange("q (j u s) -> q j s u", j=2, u=2),
                )
            else:
                nc.scalar.copy(out=yT[:, cols_of(key)], in_=bank[:])

        def x_quant(c):
            cols = slice(X_OF[c][0], X_OF[c][0] + X_OF[c][1])
            nc.vector.quantize_mx(out=xc[:, cols].bitcast(FP8X4), scales=xs[:, cols], in_=xg[c][:].bitcast(BF16))

        def shared(unit):
            return unit[0] in V_CHUNKS and unit[1:] in SHARED

        def regroup(unit):
            width = CHUNKS[unit[0]][1] - (S_COLS if shared(unit) else 0)
            if unit not in hg:
                hg[unit] = work.tile([P, CHUNKS[unit[0]][1], 4], BF16, tag="hg", name="hg", align_bytes=64, bufs=4)
            nc.vector.tensor_copy(
                out=hg[unit][:, 0:width, :].rearrange("p (c i) t -> p c t i", i=8),
                in_=hc[unit][:, :, 0:width].rearrange("p t (c i) -> p c t i", i=8),
            )

        def regroup_on_scalar(unit):
            width = CHUNKS[unit[0]][1]
            hg[unit] = work.tile([P, width, 4], BF16, tag="hg", name="hg", align_bytes=64, bufs=4)
            nc.scalar.copy(
                out=hg[unit][:, width - S_COLS : width, :].rearrange("p (c i) t -> p c t i", i=8),
                in_=hc[unit][:, :, width - S_COLS : width].rearrange("p t (c i) -> p c t i", i=8),
            )

        def quant(unit):
            c = unit[0]
            grouped = hp[c] if c in V_CHUNKS and unit[1:] == (LV, 1) else hg[unit]
            hq[unit] = work.tile([P, CHUNKS[c][1]], U32, tag="hq", name="hq", align_bytes=64, bufs=4)
            hs[unit] = work.tile([P, CHUNKS[c][1]], U8, tag="hs", name="hs", align_bytes=64, bufs=4)
            nc.vector.quantize_mx(
                out=hq[unit][:].bitcast(FP8X4), scales=hs[unit][:], in_=grouped[:].rearrange("p c t -> p (c t)")
            )

        def fill_v(c, b):
            pb[(c, b)] = psum.tile([P, BANK], F32, tag="v", name="pb")
            lo = CHUNKS[c][0] + P * b
            for t in range(4):
                mx1(pb[(c, b)][:, P * t : P * (t + 1)], LV, 512 + P * t, slice(lo, lo + P))

        def empty_v(c, b):
            if b == 0:
                hp[c] = work.tile([P, CHUNKS[c][1], 4], BF16, tag="hp", name="hp", align_bytes=64)
            nc.vector.tensor_tensor(
                out=hp[c][:, P * b : P * (b + 1), :].rearrange("p (n i) t -> p n t i", i=4),
                in0=pb[(c, b)][:].rearrange("p (t n i) -> p n t i", t=4, i=4),
                in1=bias_sb[:, 4:8].unsqueeze(1).unsqueeze(3).to_broadcast([P, P // 4, 4, 4]),
                op=ALU.add,
            )

        def fill_b(unit):
            c, h, g = unit
            pb[unit] = psum.tile([P, CHUNKS[c][1]], F32, tag="v", name="pb")
            mx1(pb[unit][:], h, 512 * g + 3 * P, cols_of(c))

        def empty_b(unit):
            c, h, g = unit
            col = 8 * h + 4 * g + 3
            nc.vector.tensor_scalar(
                out=hc[unit][:, 3, :], in0=pb[unit][:], scalar1=bias_sb[:, col : col + 1], scalar2=0.0,
                op0=ALU.add, op1=ALU.max,
            )

        def relu_v(c):
            flat = hp[c][:].rearrange("p c t -> p (c t)")
            nc.vector.tensor_scalar(out=flat, in0=flat, scalar1=0.0, scalar2=None, op0=ALU.max)

        def stage2(unit):
            c, h, g = unit
            opens = (c, h) not in left
            if opens:
                left[(c, h)] = 2
                acc[(c, h)] = psum.tile([P, CHUNKS[c][1]], F32, tag="acc%d" % h, name="acc")
            left[(c, h)] -= 1
            cols = slice(Y_DIM * g, Y_DIM * (g + 1))
            nc.tensor.matmul_mx(
                out=acc[(c, h)][:],
                lhsT=w2c[h][:, cols].bitcast(FP8X4),
                lhsT_scale=w2s[h][:, cols],
                rhs=hq[unit][:].bitcast(FP8X4),
                rhs_scale=hs[unit][:],
                start=opens,
                stop=left[(c, h)] == 0,
            )

        def ep_tile(c, what):
            ep[(c, what)] = work.tile([P, CHUNKS[c][1]], F32, tag="ep_" + what, name="ep_" + what)
            return ep[(c, what)]

        def tanh_lv(c):
            nc.scalar.activation(out=ep_tile(c, "th")[:], in_=acc[(c, LV)][:], func=ACT.Tanh, bias=b2_sb[LV][:])

        def exp_w(c):
            nc.scalar.activation(out=ep_tile(c, "w")[:], in_=ep[(c, "th")][:], func=ACT.Exp, scale=-1.0)

        def sq_e(c):
            nc.scalar.activation(out=ep_tile(c, "e2")[:], in_=acc[(c, MU)][:], func=ACT.Square, bias=stat2[:, 0:1])

        def diff_d(c):
            nc.vector.scalar_tensor_tensor(
                out=ep_tile(c, "d")[:], in0=acc[(c, MU)][:], scalar=b2_sb[MU][:],
                in1=yT[:, cols_of(c)], op0=ALU.add, op1=ALU.subtract,
            )

        def sq_d(c):
            nc.scalar.activation(out=ep_tile(c, "d2")[:], in_=ep[(c, "d")][:], func=ACT.Square)

        def sq_d_on_vector(c):
            nc.vector.tensor_tensor(out=ep_tile(c, "d2")[:], in0=ep[(c, "d")][:], in1=ep[(c, "d")][:], op=ALU.mult)

        def term_q(c):
            nc.vector.scalar_tensor_tensor(
                out=ep_tile(c, "q")[:], in0=ep[(c, "e2")][:], scalar=stat2[:, 24:25], in1=ep[(c, "w")][:],
                op0=ALU.add, op1=ALU.mult,
            )

        def term_p(c):
            nc.vector.tensor_tensor(out=ep_tile(c, "p")[:], in0=ep[(c, "d2")][:], in1=ep[(c, "w")][:], op=ALU.mult)

        def sums_over_d(c, what, cols=None):
            o = 0 if what == "p" else 1
            row, col = divmod(CHUNKS[c][0], BANK)
            row += N_ROWS * o
            if misc["sums"] == 0:
                misc["r"] = psum.tile([P, BANK], F32, tag="mr", name="r_ps")
            cols = cols or slice(0, CHUNKS[c][1])
            misc["sums"] += cols.stop - cols.start
            nc.tensor.matmul(
                out=misc["r"][:, col + cols.start : col + cols.stop], lhsT=sel[o][:, P - row : 2 * P - row],
                rhs=ep[(c, what)][:, cols],
                start=(misc["sums"] == cols.stop - cols.start), stop=(misc["sums"] == 2 * N_S),
            )

        def gram(part):
            if part == 0:
                misc["g"] = psum.tile([P, BANK], F32, tag="mr", name="g_ps")
            for i in range(8):
                j = 8 * part + i
                nc.tensor.matmul(
                    out=misc["g"][:, 0 : Y_DIM + 2], lhsT=y_sb[:, j, 0:Y_DIM], rhs=y_sb[:, j, 0 : Y_DIM + 2],
                    start=(j == 0), stop=(j == JT - 1),
                )

        def statistics():
            g_ps = misc["g"]
            gd = work.tile([P, P], F32, tag="gd", name="gd")
            nc.vector.tensor_tensor(out=gd[:], in0=g_ps[:, 0:P], in1=ident_f[:], op=ALU.mult)
            nc.vector.tensor_scalar(
                out=stat[:, 1:2], in0=g_ps[:, P : P + 1], scalar1=inv_n, scalar2=None, op0=ALU.mult
            )
            nc.vector.reduce_sum(out=stat[:, 0:1], in_=gd[:], axis=AX.X)
            nc.gpsimd.tensor_tensor(out=stat2[:, 0:1], in0=b2_sb[MU][:], in1=stat[:, 1:2], op=ALU.subtract)
            nc.gpsimd.tensor_tensor(out=stat2[:, 8:9], in0=stat[:, 1:2], in1=stat[:, 1:2], op=ALU.mult)
            nc.gpsimd.tensor_scalar(out=stat2[:, 16:17], in0=stat[:, 0:1], scalar1=inv_n, scalar2=None, op0=ALU.mult)
            nc.gpsimd.tensor_tensor(out=stat2[:, 24:25], in0=stat2[:, 16:17], in1=stat2[:, 8:9], op=ALU.subtract)

        for half in range(CHUNKS[0][1] // 256):
            fill(("x", 0, half))
            empty(("x", 0, half))
        bt_ps = psum.tile([P, P], BF16, tag="v", name="bt_ps")
        nc.tensor.transpose(bt_ps[:], braw[:], ident_b[:])
        warm_ps = psum.tile([P, BANK], F32, tag="mr", name="warm_ps")
        for n in range(3):
            nc.tensor.matmul(out=warm_ps[:], lhsT=ident_b[:], rhs=x_sb[:, 0:BANK], start=True, stop=True)
        wgf0 = work.tile([P, 256, 4], BF16, tag="wgf", name="wgf0", align_bytes=64)
        nc.vector.tensor_copy(
            out=wgf0[:].rearrange("p (c i) t -> p c t i", i=8), in_=w1first[0][:].rearrange("p t (c i) -> p c t i", i=8)
        )
        wgf1 = work.tile([P, 256, 4], BF16, tag="wgf", name="wgf1", align_bytes=64)
        nc.vector.tensor_copy(
            out=wgf1[:].rearrange("p (c i) t -> p c t i", i=8), in_=w1first[1][:].rearrange("p t (c i) -> p c t i", i=8)
        )
        nc.vector.quantize_mx(
            out=w1c[LV][:, 0 : 256].bitcast(FP8X4), scales=w1s[LV][:, 0 : 256],
            in_=wgf0[:].rearrange("p c t -> p (c t)"),
        )
        nc.vector.tensor_copy(out=bias_sb[:], in_=bt_ps[:, 0:16])
        x_quant(0)
        nc.vector.quantize_mx(
            out=w1c[LV][:, 256 : 512].bitcast(FP8X4), scales=w1s[LV][:, 256 : 512],
            in_=wgf1[:].rearrange("p c t -> p (c t)"),
        )
        wg1 = w1_regroup(LV, 1, "v")

        n_steps = 4 * NC
        step_banks = []
        regroup_at = {}
        relu_at = {}
        for c in range(NC):
            if c in V_CHUNKS:
                units = [(c, LV, 0), (c, MU, 0), (c, MU, 1)]
                offsets = (2, 3, 5)
                relu_at[4 * c + 4] = c
            else:
                units = [(c, h, g) for h in range(2) for g in range(2)]
                offsets = (1, 2, 3, 4)
            for unit, offset in zip(units, offsets):
                regroup_at.setdefault(4 * c + offset, []).append(unit)
            banks_of_chunk = [("u", unit, t) for unit in units for t in range(4)]
            n = len(units)
            for r in range(4):
                here = banks_of_chunk[n * r : n * (r + 1)]
                if (c, r) in B_STEPS:
                    here.pop()
                if c + 1 in X_OF and r == 0:
                    here += [("x", c + 1, half) for half in range(X_OF[c + 1][1] // 256)]
                if r == 2 and c >= 1:
                    here.append(("y", c - 1, 0))
                if r == 3 and c == NC - 1:
                    here.append(("y", c, 0))
                step_banks.append(here)
        stream = [bank for here in step_banks for bank in here]
        quant_at = {}
        for s in list(regroup_at):
            for unit in regroup_at[s]:
                quant_at.setdefault(s + 1, []).append(unit)
        for s in list(relu_at):
            quant_at.setdefault(s + 1, []).append((relu_at[s], LV, 1))

        done = 0
        for n in range(RING):
            fill(stream[n])
        for s in range(n_steps + 8):
            c, r = divmod(s, 4)
            old = c - 1
            older = c - 2
            ends = 0 <= older < NC
            here = step_banks[s] if s < n_steps else []

            if r == 0 and ends and c >= NC:
                diff_d(older)
                sq_e(older)
            if s == 0:
                wg2 = w1_regroup(MU, 0, "v")
                w1_quant(LV, 1, wg1)
                w1_quant(MU, 0, wg2)
            if s == 1:
                wg = w1_regroup(MU, 1, "v")
            if r == 2 and c + 1 in X_OF:
                x_quant(c + 1)
            if r == 1 and ends:
                term_q(older)
            if r == 3 and ends:
                term_p(older)
            for unit in quant_at.get(s, []):
                quant(unit)
            if s in relu_at:
                relu_v(relu_at[s])
            for unit in regroup_at.get(s, []):
                regroup(unit)
            if s == 1:
                w1_quant(MU, 1, wg)
            if s in (1, 2):
                w2g_of[s - 1] = w2_regroup(s - 1)
            if s in (2, 3):
                w2_quant(s - 2, w2g_of[s - 2])
            if s == 7:
                statistics()

            for i in range(max(4, len(here))):
                if i == 1 and r == 3 and 0 <= old < NC:
                    tanh_lv(old)
                if i == 2 and r == 0 and ends and c < NC:
                    sq_e(older)
                if i < len(here):
                    empty(here[i])
                    done += 1
                    if done + RING <= len(stream):
                        fill(stream[done + RING - 1])
                if i == 0 and c in V_CHUNKS and P * r < CHUNKS[c][1]:
                    fill_v(c, r)
                if i == 1 and (c, r) in B_STEPS:
                    fill_b((c, r // 2, r % 2))
                if i == 1:
                    for unit in quant_at.get(s - 1, []):
                        stage2(unit)
                if i == 3 and r == 2 and ends and older not in HALVED:
                    sums_over_d(older, "q")
                if i == 3 and r == 1 and ends and older in HALVED:
                    sums_over_d(older, "q", slice(0 * 256, 0 * 256 + 256))
                if i == 2 and r == 2 and ends and older in HALVED:
                    sums_over_d(older, "q", slice(1 * 256, 1 * 256 + 256))
                if i == 3 and r == 3 and ends and older not in HALVED:
                    sums_over_d(older, "p")
                if i == 1 and r == 3 and ends and older in HALVED:
                    sums_over_d(older, "p", slice(0 * 256, 0 * 256 + 256))
                if i == 3 and r == 3 and ends and older in HALVED:
                    sums_over_d(older, "p", slice(1 * 256, 1 * 256 + 256))
                if s in (5, 6) and i == 2:
                    gram(2 * (s - 5))
                    gram(2 * (s - 5) + 1)
            for item in here:
                if item[0] == "u" and item[2] == 3 and shared(item[1]):
                    regroup_on_scalar(item[1])
            if r == 3 and 0 <= old < NC:
                exp_w(old)
            if r == 1 and ends:
                sq_d(older)

            if r == 0 and ends and c < NC:
                diff_d(older)
            if c in V_CHUNKS and P * r < CHUNKS[c][1]:
                empty_v(c, r)
            if (c, r) in B_STEPS:
                empty_b((c, r // 2, r % 2))

        nc.vector.tensor_copy(
            out=r_sb[:].rearrange("c (s j) -> c s j", j=4),
            in_=misc["r"][0 : 2 * N_ROWS, :].rearrange("c (j s) -> c s j", j=4),
        )
        nc.sync.dma_start(out=out_0.rearrange("(c i) -> c i", i=BANK), in_=r_sb[0:N_ROWS, :])
        nc.sync.dma_start(out=out_1.rearrange("(c i) -> c i", i=BANK), in_=r_sb[N_ROWS : 2 * N_ROWS, :])
